import numpy as np
import ml_dtypes


def mxq(x, axis, fmt="e4m3"):
    dtype, down = {"e4m3": (ml_dtypes.float8_e4m3fn, 7), "e5m2": (ml_dtypes.float8_e5m2, 14)}[fmt]
    v = np.moveaxis(np.asarray(x, np.float32).astype(ml_dtypes.bfloat16).astype(np.float64), axis, -1)
    blocks = v.reshape(v.shape[:-1] + (-1, 32))
    amax = np.abs(blocks).max(-1, keepdims=True)
    byte = np.maximum(np.where(amax > 0, np.frexp(amax)[1] - 1 + 127, 0) - down, 1)
    scale = np.exp2(byte - 127.0)
    codes = (blocks / scale).astype(np.float32).astype(dtype).astype(np.float64)
    return np.moveaxis((codes * scale).reshape(v.shape), -1, axis)


WIDE = False


def mx_kscale(k):
    if not WIDE:
        return np.ones(k)
    levels = np.array([10, -10, 5, -5, 0])
    a = np.random.permutation(np.resize(levels, k // 512 * 4)).reshape(k // 512, 4)
    idx = np.arange(k)
    return np.exp2(a[idx // 512, idx % 128 // 32])


BF16 = ml_dtypes.bfloat16


def bf(x):
    return np.asarray(x, np.float32).astype(BF16)


def f64(x):
    return np.asarray(x).astype(np.float64)


E2M1 = np.array([0.0, 0.5, 1.0, 1.5, 2.0, 3.0, 4.0, 6.0, -0.0, -0.5, -1.0, -1.5, -2.0, -3.0, -4.0, -6.0])


def pack_weight(w, fmt):
    k, n = w.shape
    w = f64(bf(w)).reshape(k // 32, 32, n)
    amax = np.abs(w).max(1)
    if fmt == "e4m3":
        byte = np.frexp(amax)[1] - 1 + 127 - 7
    else:
        mant, ex = np.frexp(amax / 6.0)
        byte = np.where(mant > 0.5, ex, ex - 1) + 127
    byte = np.clip(np.where(amax > 0, byte, 1), 1, 254)
    scaled = (w * np.exp2(127.0 - byte)[:, None, :]).reshape(k, n).astype(np.float32)
    by_word = np.ascontiguousarray(scaled.reshape(k // 512, 128, 4, n).transpose(0, 1, 3, 2))
    if fmt == "e4m3":
        words = by_word.astype(ml_dtypes.float8_e4m3fn).view(np.uint8)
    else:
        c = by_word.astype(ml_dtypes.float4_e2m1fn).view(np.uint8) & 0xF
        words = c[..., 0::2] | (c[..., 1::2] << 4)
    return np.ascontiguousarray(words), np.ascontiguousarray(byte.astype(np.uint8).reshape(k // 512, 16, n))


def unpack_weight(words, scales, fmt):
    g, p, n, _ = words.shape
    if fmt == "e4m3":
        vals = np.ascontiguousarray(words).view(ml_dtypes.float8_e4m3fn).astype(np.float64)
    else:
        nib = np.empty((g, p, n, 4), np.uint8)
        nib[..., 0::2] = words & 0xF
        nib[..., 1::2] = words >> 4
        vals = E2M1[nib]
    vals = vals * np.repeat(np.exp2(scales.astype(np.float64) - 127.0), 8, axis=1)[..., None]
    return vals.transpose(0, 1, 3, 2).reshape(g * 512, n)

def pack4(w):
    words, scales = pack_weight(w, "e2m1")
    return words.reshape(words.shape[0], 128, -1), scales


def unpack4(words, scales):
    return unpack_weight(words.reshape(words.shape[0], 128, -1, 2), scales, "e2m1")


B, N, DIM, H, DH = 2, 2048, 1024, 4, 96
D1 = DH // 3


def rotate_half(t):
    d = t.shape[-1]
    t1, t2 = t[..., : (d + 1) // 2], t[..., (d + 1) // 2:]
    return np.concatenate((-t2, t1), axis=-1)


def apply_rope(t, freqs):
    return t * np.cos(freqs) + rotate_half(t) * np.sin(freqs)


def rope3(t, fs):
    return np.concatenate([apply_rope(ts, f) for ts, f in zip(np.split(t, (D1, 2 * D1), axis=-1), fs)], axis=-1)


def setup_inputs():
    s = mx_kscale(DIM)
    x = bf(np.random.standard_normal((B, N, DIM)) * s)
    f1 = bf(np.random.uniform(0.0, 1.0, (N, D1)))
    f2 = bf(np.random.uniform(0.0, 1.0, (N, D1)))
    f3 = bf(np.random.uniform(0.0, 1.0, (N, D1)))
    words, scales = pack4(np.random.standard_normal((DIM, 3 * H * DH)) / np.sqrt(DIM) / s[:, None])
    return {"x": x, "f1": f1, "f2": f2, "f3": f3, "Wqkv_words": words, "Wqkv_scales": scales}


def reference(x, f1, f2, f3, Wqkv_words, Wqkv_scales):
    qkv = mxq(f64(x), 2, "e4m3") @ unpack4(Wqkv_words, Wqkv_scales)
    q, k, v = np.split(qkv, 3, axis=-1)
    to_heads = lambda t: t.reshape(B, N, H, DH).transpose(0, 2, 1, 3)
    q, k, v = to_heads(q), to_heads(k), to_heads(v)
    fs = (f64(f1), f64(f2), f64(f3))
    return rope3(q, fs), rope3(k, fs), v

@@ -1,0 +1,214 @@
+import math
+from contextlib import ExitStack
+
+import concourse.mybir as mybir
+from concourse.masks import make_identity
+
+F32 = mybir.dt.float32
+BF16 = mybir.dt.bfloat16
+I32 = mybir.dt.int32
+U8 = mybir.dt.uint8
+U32 = mybir.dt.uint32
+FP8X4 = mybir.dt.float8_e4m3fn_x4
+FP4X4 = mybir.dt.float4_e2m1fn_x4
+MULT = mybir.AluOpType.mult
+ADD = mybir.AluOpType.add
+SIN = mybir.ActivationFunctionType.Sin
+
+P = 128
+BATCH, TOKENS, DIM = 2, 2048, 1024
+HEADS, HEAD_DIM = 4, 96
+AXES, AXIS_DIM = 3, 32
+HALF = AXIS_DIM // 2
+PART = HEADS * HEAD_DIM
+PACK = 4
+PASSES = DIM // (P * PACK)
+WORDS = P * PACK // 2
+CHUNK = 128
+ROWS = TOKENS // P
+PAIR = 2
+GROUP = 4
+STEPS = BATCH * ROWS // PAIR
+
+FLOPS = 2 * BATCH * TOKENS * DIM * 3 * PART
+
+
+def tile_attention_pa_t_kernel(
+    tc, x, f1, f2, f3, Wqkv_words, Wqkv_scales, out_0, out_1, out_2
+):
+    nc = tc.nc
+    x_rows = x.rearrange("b (p i) k -> b p i k", i=ROWS)
+    out_rows = [o.rearrange("b h (p i) d -> b p h i d", i=ROWS) for o in (out_0, out_1, out_2)]
+
+    with ExitStack() as ctx:
+        const = ctx.enter_context(tc.tile_pool(name="const", bufs=1))
+        x_pool = ctx.enter_context(tc.tile_pool(name="x_pool", bufs=STEPS))
+        stage = ctx.enter_context(tc.tile_pool(name="stage", bufs=2))
+        results = ctx.enter_context(tc.tile_pool(name="results", bufs=3))
+        psum_t = ctx.enter_context(tc.psum_pool(name="psum_t", bufs=PAIR))
+        psum_o = ctx.enter_context(tc.psum_pool(name="psum_o", bufs=PAIR))
+        ctx.enter_context(tc.manual_schedule())
+
+        ident = const.tile([P, P], F32, name="ident")
+        make_identity(nc, ident[:])
+
+        w_scales = const.tile([P, PASSES, 3 * PART], U8, name="w_scales", align_bytes=64)
+        nc.vector.memset(w_scales[:].bitcast(I32), 0)
+        w_words = const.tile([P, PASSES, 2 * 3 * PART], U8, name="w_words", align_bytes=64)
+        angles = const.tile([P, AXES, ROWS, AXIS_DIM], BF16, name="angles")
+        table = const.tile([P, ROWS, 2, HEAD_DIM], F32, name="table")
+
+        x_tiles = {}
+
+        def load_x(s):
+            b, i0 = divmod(s * PAIR, ROWS)
+            x_tiles[s] = x_pool.tile([P, PAIR, DIM], BF16, name="x_pair")
+            nc.sync.dma_start(out=x_tiles[s][:], in_=x_rows[b][:, i0 : i0 + PAIR, :])
+
+        load_x(0)
+        for g in range(PASSES):
+            nc.sync.dma_start(out=w_words[:, g, :].bitcast(I32), in_=Wqkv_words[g].bitcast(I32))
+        scale_rows = Wqkv_scales.rearrange("g (q r) n -> r q g n", r=4)
+        for r in range(4):
+            nc.sync.dma_start(
+                out=w_scales[r:P:32, :, :].bitcast(I32), in_=scale_rows[r].bitcast(I32)
+            )
+        for a, f in enumerate((f1, f2, f3)):
+            nc.sync.dma_start(out=angles[:, a, :, :], in_=f.rearrange("(p i) e -> p i e", i=ROWS))
+        for s in range(1, STEPS):
+            load_x(s)
+
+        def make_table(i_lo, i_hi):
+            f_in = angles[:, :, i_lo:i_hi, :]
+            nc.scalar.activation(
+                out=table[:, i_lo:i_hi, 0, :].rearrange("p i (a e) -> p i a e", a=AXES),
+                in_=f_in.rearrange("p a i e -> p i a e"),
+                func=SIN,
+                bias=math.pi / 2,
+                scale=-1.0,
+            )
+            f_halves = f_in.rearrange("p a i (f e) -> p i a f e", f=2)
+            s_halves = table[:, i_lo:i_hi, 1, :].rearrange("p i (a f e) -> p i a f e", a=AXES, f=2)
+            nc.scalar.activation(
+                out=s_halves[:, :, :, 0, :], in_=f_halves[:, :, :, 1, :], func=SIN, scale=1.0
+            )
+            nc.scalar.activation(
+                out=s_halves[:, :, :, 1, :], in_=f_halves[:, :, :, 0, :], func=SIN, scale=-1.0
+            )
+
+        flipped, grouped, codes, x_scales, banks, rotated, v_rows = {}, {}, {}, {}, {}, {}, {}
+
+        def transpose(s):
+            for e in range(PAIR):
+                flipped[s, e] = psum_t.tile([P, PASSES, 2, P], F32, name="flipped")
+                words = x_tiles[s][:, e, :].bitcast(F32)
+                for g in range(PASSES):
+                    for u in range(2):
+                        nc.tensor.transpose(
+                            flipped[s, e][:, g, u, :],
+                            words[:, WORDS * g + u : WORDS * (g + 1) : 2],
+                            ident[:],
+                        )
+
+        def regroup(s):
+            grouped[s] = stage.tile(
+                [P, PAIR, PASSES, P, PACK], BF16, name="grouped", align_bytes=64
+            )
+            for e in range(PAIR):
+                nc.scalar.copy(
+                    out=grouped[s][:, e].bitcast(F32),
+                    in_=flipped[s, e][:].rearrange("p g u r -> p g r u"),
+                )
+
+        def quantise(s):
+            codes[s] = stage.tile([P, PAIR * PASSES, P], U32, name="codes", align_bytes=64)
+            x_scales[s] = stage.tile([P, PAIR * PASSES, P], U8, name="x_scales", align_bytes=64)
+            nc.vector.quantize_mx(
+                out=codes[s][:].rearrange("p c r -> p (c r)").bitcast(FP8X4),
+                scales=x_scales[s][:].rearrange("p c r -> p (c r)"),
+                in_=grouped[s][:].rearrange("p e g r t -> p (e g r t)"),
+            )
+
+        def project(s, e):
+            for part in range(3):
+                bank = psum_o.tile([P, PART], F32, name="bank%d" % part)
+                banks[s, e, part] = bank
+                for c in range(PART // CHUNK):
+                    col = part * PART + c * CHUNK
+                    for g in range(PASSES):
+                        nc.tensor.matmul_mx(
+                            out=bank[:, c * CHUNK : (c + 1) * CHUNK],
+                            lhsT=codes[s][:, e * PASSES + g, :].bitcast(FP8X4),
+                            lhsT_scale=x_scales[s][:, e * PASSES + g, :],
+                            rhs=w_words[:, g, 2 * col : 2 * (col + CHUNK)].bitcast(FP4X4),
+                            rhs_scale=w_scales[:, g, col : col + CHUNK],
+                            start=(g == 0),
+                            stop=(g == PASSES - 1),
+                        )
+
+        def rotate(s, e):
+            n = s * PAIR + e
+            if n % GROUP == 0:
+                rotated[n // GROUP] = results.tile(
+                    [P, 2, 2 * HEADS, GROUP, HEAD_DIM], F32, name="rotated"
+                )
+            both = [P, 2, HEADS, HEAD_DIM]
+            for part in range(2):
+                by_head = banks[s, e, part][:].rearrange("p (h d) -> p h d", h=HEADS)
+                nc.vector.tensor_tensor(
+                    out=rotated[n // GROUP][:, :, part * HEADS : (part + 1) * HEADS, n % GROUP, :],
+                    in0=by_head.unsqueeze(1).to_broadcast(both),
+                    in1=table[:, n % ROWS, :, :].unsqueeze(2).to_broadcast(both),
+                    op=MULT,
+                )
+
+        def keep_v(s, e):
+            n = s * PAIR + e
+            if n % GROUP == 0:
+                v_rows[n // GROUP] = results.tile([P, HEADS, GROUP, HEAD_DIM], F32, name="v_rows")
+            nc.scalar.copy(
+                out=v_rows[n // GROUP][:, :, n % GROUP, :],
+                in_=banks[s, e, 2][:].rearrange("p (h d) -> p h d", h=HEADS),
+            )
+
+        def finish(m):
+            halves = rotated[m][:].rearrange(
+                "p t c i (a f e) -> p t c (i a) f e", a=AXES, f=2
+            )
+            for f in range(2):
+                nc.gpsimd.tensor_tensor(
+                    out=halves[:, 0, :, :, f, :],
+                    in0=halves[:, 0, :, :, f, :],
+                    in1=halves[:, 1, :, :, 1 - f, :],
+                    op=ADD,
+                )
+            b, i0 = divmod(m * GROUP, ROWS)
+            for part in range(2):
+                nc.sync.dma_start(
+                    out=out_rows[part][b][:, :, i0 : i0 + GROUP, :],
+                    in_=rotated[m][:, 0, part * HEADS : (part + 1) * HEADS, :, :],
+                )
+            nc.sync.dma_start(out=out_rows[2][b][:, :, i0 : i0 + GROUP, :], in_=v_rows[m][:])
+
+        transpose(0)
+        regroup(0)
+        quantise(0)
+        make_table(0, GROUP)
+        transpose(1)
+        regroup(1)
+        make_table(GROUP, ROWS)
+        for s in range(STEPS):
+            project(s, 0)
+            project(s, 1)
+            if s + 2 < STEPS:
+                transpose(s + 2)
+            rotate(s, 0)
+            if s + 1 < STEPS:
+                quantise(s + 1)
+            rotate(s, 1)
+            keep_v(s, 0)
+            keep_v(s, 1)
+            if s + 2 < STEPS:
+                regroup(s + 2)
+            if (s + 1) * PAIR % GROUP == 0:
+                finish((s + 1) * PAIR // GROUP - 1)

@@ -23,7 +23,6 @@ HALF = AXIS_DIM // 2
 PART = HEADS * HEAD_DIM
 PACK = 4
 PASSES = DIM // (P * PACK)
-WORDS = P * PACK // 2
 CHUNK = 128
 ROWS = TOKENS // P
 PAIR = 2
@@ -96,18 +95,25 @@ def tile_attention_pa_t_kernel(
                 out=s_halves[:, :, :, 1, :], in_=f_halves[:, :, :, 0, :], func=SIN, scale=-1.0
             )
 
-        flipped, grouped, codes, x_scales, banks, rotated, v_rows = {}, {}, {}, {}, {}, {}, {}
+        ordered, flipped, grouped, codes, x_scales = {}, {}, {}, {}, {}
+        banks, rotated, v_rows = {}, {}, {}
+
+        def sort_words(s):
+            ordered[s] = stage.tile([P, PAIR * PASSES, 2, P], F32, name="ordered")
+            nc.scalar.copy(
+                out=ordered[s][:],
+                in_=x_tiles[s][:]
+                .bitcast(F32)
+                .rearrange("p e (g q u) -> p (e g) u q", g=PASSES, u=2),
+            )
 
         def transpose(s):
             for e in range(PAIR):
                 flipped[s, e] = psum_t.tile([P, PASSES, 2, P], F32, name="flipped")
-                words = x_tiles[s][:, e, :].bitcast(F32)
                 for g in range(PASSES):
                     for u in range(2):
                         nc.tensor.transpose(
-                            flipped[s, e][:, g, u, :],
-                            words[:, WORDS * g + u : WORDS * (g + 1) : 2],
-                            ident[:],
+                            flipped[s, e][:, g, u, :], ordered[s][:, e * PASSES + g, u, :], ident[:]
                         )
 
         def regroup(s):
@@ -171,31 +177,38 @@ def tile_attention_pa_t_kernel(
                 in_=banks[s, e, 2][:].rearrange("p (h d) -> p h d", h=HEADS),
             )
 
-        def finish(m):
-            halves = rotated[m][:].rearrange(
+        def finish(engine, n_lo, n_hi):
+            m, lo = divmod(n_lo, GROUP)
+            hi = lo + n_hi - n_lo
+            halves = rotated[m][:, :, :, lo:hi, :].rearrange(
                 "p t c i (a f e) -> p t c (i a) f e", a=AXES, f=2
             )
             for f in range(2):
-                nc.gpsimd.tensor_tensor(
+                engine.tensor_tensor(
                     out=halves[:, 0, :, :, f, :],
                     in0=halves[:, 0, :, :, f, :],
                     in1=halves[:, 1, :, :, 1 - f, :],
                     op=ADD,
                 )
-            b, i0 = divmod(m * GROUP, ROWS)
+            b, i0 = divmod(n_lo, ROWS)
             for part in range(2):
                 nc.sync.dma_start(
-                    out=out_rows[part][b][:, :, i0 : i0 + GROUP, :],
-                    in_=rotated[m][:, 0, part * HEADS : (part + 1) * HEADS, :, :],
+                    out=out_rows[part][b][:, :, i0 : i0 + hi - lo, :],
+                    in_=rotated[m][:, 0, part * HEADS : (part + 1) * HEADS, lo:hi, :],
                 )
-            nc.sync.dma_start(out=out_rows[2][b][:, :, i0 : i0 + GROUP, :], in_=v_rows[m][:])
+            nc.sync.dma_start(
+                out=out_rows[2][b][:, :, i0 : i0 + hi - lo, :], in_=v_rows[m][:, :, lo:hi, :]
+            )
 
+        sort_words(0)
+        sort_words(1)
         transpose(0)
         regroup(0)
         quantise(0)
         make_table(0, GROUP)
         transpose(1)
         regroup(1)
+        sort_words(2)
         make_table(GROUP, ROWS)
         for s in range(STEPS):
             project(s, 0)
@@ -210,5 +223,12 @@ def tile_attention_pa_t_kernel(
             keep_v(s, 1)
             if s + 2 < STEPS:
                 regroup(s + 2)
-            if (s + 1) * PAIR % GROUP == 0:
-                finish((s + 1) * PAIR // GROUP - 1)
+            if s + 3 < STEPS:
+                sort_words(s + 3)
+            done = (s + 1) * PAIR
+            if s == STEPS - 1:
+                finish(nc.vector, done - PAIR, done)
+            elif s == STEPS - 2:
+                finish(nc.gpsimd, done - PAIR, done)
+            elif done % GROUP == 0:
+                finish(nc.gpsimd, done - GROUP, done)

@@ -23,10 +23,12 @@ HALF = AXIS_DIM // 2
 PART = HEADS * HEAD_DIM
 PACK = 4
 PASSES = DIM // (P * PACK)
+WORDS = P * PACK // 2
 CHUNK = 128
 ROWS = TOKENS // P
 PAIR = 2
 GROUP = 4
+GPSIMD_TILES = 3
 STEPS = BATCH * ROWS // PAIR
 
 FLOPS = 2 * BATCH * TOKENS * DIM * 3 * PART
@@ -95,25 +97,18 @@ def tile_attention_pa_t_kernel(
                 out=s_halves[:, :, :, 1, :], in_=f_halves[:, :, :, 0, :], func=SIN, scale=-1.0
             )
 
-        ordered, flipped, grouped, codes, x_scales = {}, {}, {}, {}, {}
-        banks, rotated, v_rows = {}, {}, {}
-
-        def sort_words(s):
-            ordered[s] = stage.tile([P, PAIR * PASSES, 2, P], F32, name="ordered")
-            nc.scalar.copy(
-                out=ordered[s][:],
-                in_=x_tiles[s][:]
-                .bitcast(F32)
-                .rearrange("p e (g q u) -> p (e g) u q", g=PASSES, u=2),
-            )
+        flipped, grouped, codes, x_scales, banks, rotated, v_rows = {}, {}, {}, {}, {}, {}, {}
 
         def transpose(s):
             for e in range(PAIR):
                 flipped[s, e] = psum_t.tile([P, PASSES, 2, P], F32, name="flipped")
+                words = x_tiles[s][:, e, :].bitcast(F32)
                 for g in range(PASSES):
                     for u in range(2):
                         nc.tensor.transpose(
-                            flipped[s, e][:, g, u, :], ordered[s][:, e * PASSES + g, u, :], ident[:]
+                            flipped[s, e][:, g, u, :],
+                            words[:, WORDS * g + u : WORDS * (g + 1) : 2],
+                            ident[:],
                         )
 
         def regroup(s):
@@ -177,9 +172,7 @@ def tile_attention_pa_t_kernel(
                 in_=banks[s, e, 2][:].rearrange("p (h d) -> p h d", h=HEADS),
             )
 
-        def finish(engine, n_lo, n_hi):
-            m, lo = divmod(n_lo, GROUP)
-            hi = lo + n_hi - n_lo
+        def add_up(engine, m, lo, hi):
             halves = rotated[m][:, :, :, lo:hi, :].rearrange(
                 "p t c i (a f e) -> p t c (i a) f e", a=AXES, f=2
             )
@@ -190,32 +183,32 @@ def tile_attention_pa_t_kernel(
                     in1=halves[:, 1, :, :, 1 - f, :],
                     op=ADD,
                 )
-            b, i0 = divmod(n_lo, ROWS)
+
+        def store(m):
+            b, i0 = divmod(m * GROUP, ROWS)
             for part in range(2):
                 nc.sync.dma_start(
-                    out=out_rows[part][b][:, :, i0 : i0 + hi - lo, :],
-                    in_=rotated[m][:, 0, part * HEADS : (part + 1) * HEADS, lo:hi, :],
+                    out=out_rows[part][b][:, :, i0 : i0 + GROUP, :],
+                    in_=rotated[m][:, 0, part * HEADS : (part + 1) * HEADS, :, :],
                 )
-            nc.sync.dma_start(
-                out=out_rows[2][b][:, :, i0 : i0 + hi - lo, :], in_=v_rows[m][:, :, lo:hi, :]
-            )
+            nc.sync.dma_start(out=out_rows[2][b][:, :, i0 : i0 + GROUP, :], in_=v_rows[m][:])
 
-        sort_words(0)
-        sort_words(1)
         transpose(0)
         regroup(0)
         quantise(0)
         make_table(0, GROUP)
         transpose(1)
         regroup(1)
-        sort_words(2)
         make_table(GROUP, ROWS)
         for s in range(STEPS):
             project(s, 0)
             project(s, 1)
             if s + 2 < STEPS:
                 transpose(s + 2)
+            m, first = divmod(s * PAIR, GROUP)
             rotate(s, 0)
+            if first + 1 == GPSIMD_TILES:
+                add_up(nc.gpsimd, m, 0, GPSIMD_TILES)
             if s + 1 < STEPS:
                 quantise(s + 1)
             rotate(s, 1)
@@ -223,12 +216,6 @@ def tile_attention_pa_t_kernel(
             keep_v(s, 1)
             if s + 2 < STEPS:
                 regroup(s + 2)
-            if s + 3 < STEPS:
-                sort_words(s + 3)
-            done = (s + 1) * PAIR
-            if s == STEPS - 1:
-                finish(nc.vector, done - PAIR, done)
-            elif s == STEPS - 2:
-                finish(nc.gpsimd, done - PAIR, done)
-            elif done % GROUP == 0:
-                finish(nc.gpsimd, done - GROUP, done)
+            if first + PAIR == GROUP:
+                add_up(nc.vector, m, GPSIMD_TILES, GROUP)
+                store(m)

@@ -28,8 +28,8 @@ CHUNK = 128
 ROWS = TOKENS // P
 PAIR = 2
 GROUP = 4
-GPSIMD_TILES = 3
-STEPS = BATCH * ROWS // PAIR
+TILES = BATCH * ROWS
+STEPS = TILES // PAIR
 
 FLOPS = 2 * BATCH * TOKENS * DIM * 3 * PART
 
@@ -50,14 +50,22 @@ def tile_attention_pa_t_kernel(
         psum_o = ctx.enter_context(tc.psum_pool(name="psum_o", bufs=PAIR))
         ctx.enter_context(tc.manual_schedule())
 
+        angles = const.tile([P, AXES, ROWS, AXIS_DIM], BF16, name="angles")
+        for a, f in enumerate((f1, f2, f3)):
+            nc.gpsimd.dma_start(
+                out=angles[:, a, :, :], in_=f.rearrange("(p i) e -> p i e", i=ROWS)
+            )
         ident = const.tile([P, P], F32, name="ident")
         make_identity(nc, ident[:])
 
         w_scales = const.tile([P, PASSES, 3 * PART], U8, name="w_scales", align_bytes=64)
         nc.vector.memset(w_scales[:].bitcast(I32), 0)
         w_words = const.tile([P, PASSES, 2 * 3 * PART], U8, name="w_words", align_bytes=64)
-        angles = const.tile([P, AXES, ROWS, AXIS_DIM], BF16, name="angles")
         table = const.tile([P, ROWS, 2, HEAD_DIM], F32, name="table")
+
+        zero = const.tile([P, 1], F32, name="zero")
+        nc.vector.memset(zero[:], 0.0)
+        nc.scalar.activation(out=zero[:], in_=zero[:], func=SIN)
 
         x_tiles = {}
 
@@ -67,15 +75,14 @@ def tile_attention_pa_t_kernel(
             nc.sync.dma_start(out=x_tiles[s][:], in_=x_rows[b][:, i0 : i0 + PAIR, :])
 
         load_x(0)
-        for g in range(PASSES):
-            nc.sync.dma_start(out=w_words[:, g, :].bitcast(I32), in_=Wqkv_words[g].bitcast(I32))
+        nc.sync.dma_start(
+            out=w_words[:].bitcast(I32), in_=Wqkv_words.rearrange("g p n -> p g n").bitcast(I32)
+        )
         scale_rows = Wqkv_scales.rearrange("g (q r) n -> r q g n", r=4)
         for r in range(4):
             nc.sync.dma_start(
                 out=w_scales[r:P:32, :, :].bitcast(I32), in_=scale_rows[r].bitcast(I32)
             )
-        for a, f in enumerate((f1, f2, f3)):
-            nc.sync.dma_start(out=angles[:, a, :, :], in_=f.rearrange("(p i) e -> p i e", i=ROWS))
         for s in range(1, STEPS):
             load_x(s)
 
@@ -172,8 +179,9 @@ def tile_attention_pa_t_kernel(
                 in_=banks[s, e, 2][:].rearrange("p (h d) -> p h d", h=HEADS),
             )
 
-        def add_up(engine, m, lo, hi):
-            halves = rotated[m][:, :, :, lo:hi, :].rearrange(
+        def add_up(engine, s):
+            m, lo = divmod(s * PAIR, GROUP)
+            halves = rotated[m][:, :, :, lo : lo + PAIR, :].rearrange(
                 "p t c i (a f e) -> p t c (i a) f e", a=AXES, f=2
             )
             for f in range(2):
@@ -184,31 +192,32 @@ def tile_attention_pa_t_kernel(
                     op=ADD,
                 )
 
-        def store(m):
-            b, i0 = divmod(m * GROUP, ROWS)
+        def store(n, count):
+            m, lo = divmod(n, GROUP)
+            b, i0 = divmod(n, ROWS)
+            nc.sync.dma_start(
+                out=out_rows[2][b][:, :, i0 : i0 + count, :], in_=v_rows[m][:, :, lo : lo + count, :]
+            )
             for part in range(2):
                 nc.sync.dma_start(
-                    out=out_rows[part][b][:, :, i0 : i0 + GROUP, :],
-                    in_=rotated[m][:, 0, part * HEADS : (part + 1) * HEADS, :, :],
+                    out=out_rows[part][b][:, :, i0 : i0 + count, :],
+                    in_=rotated[m][:, 0, part * HEADS : (part + 1) * HEADS, lo : lo + count, :],
                 )
-            nc.sync.dma_start(out=out_rows[2][b][:, :, i0 : i0 + GROUP, :], in_=v_rows[m][:])
 
         transpose(0)
         regroup(0)
         quantise(0)
         make_table(0, GROUP)
-        transpose(1)
-        regroup(1)
-        make_table(GROUP, ROWS)
         for s in range(STEPS):
+            n = s * PAIR
             project(s, 0)
+            if s == 0:
+                transpose(1)
+                regroup(1)
             project(s, 1)
             if s + 2 < STEPS:
                 transpose(s + 2)
-            m, first = divmod(s * PAIR, GROUP)
             rotate(s, 0)
-            if first + 1 == GPSIMD_TILES:
-                add_up(nc.gpsimd, m, 0, GPSIMD_TILES)
             if s + 1 < STEPS:
                 quantise(s + 1)
             rotate(s, 1)
@@ -216,6 +225,10 @@ def tile_attention_pa_t_kernel(
             keep_v(s, 1)
             if s + 2 < STEPS:
                 regroup(s + 2)
-            if first + PAIR == GROUP:
-                add_up(nc.vector, m, GPSIMD_TILES, GROUP)
-                store(m)
+            if n % GROUP == 0 and n + GROUP < ROWS:
+                make_table(n + GROUP, n + 2 * GROUP)
+            add_up(nc.vector if s == STEPS - 1 else nc.gpsimd, s)
+            if n >= TILES - GROUP:
+                store(n, PAIR)
+            elif (n + PAIR) % GROUP == 0:
+                store(n + PAIR - GROUP, GROUP)

@@ -19,17 +19,15 @@ P = 128
 BATCH, TOKENS, DIM = 2, 2048, 1024
 HEADS, HEAD_DIM = 4, 96
 AXES, AXIS_DIM = 3, 32
-HALF = AXIS_DIM // 2
 PART = HEADS * HEAD_DIM
 PACK = 4
 PASSES = DIM // (P * PACK)
 WORDS = P * PACK // 2
 CHUNK = 128
 ROWS = TOKENS // P
+TILES = BATCH * ROWS
 PAIR = 2
 GROUP = 4
-TILES = BATCH * ROWS
-STEPS = TILES // PAIR
 
 FLOPS = 2 * BATCH * TOKENS * DIM * 3 * PART
 
@@ -43,8 +41,8 @@ def tile_attention_pa_t_kernel(
 
     with ExitStack() as ctx:
         const = ctx.enter_context(tc.tile_pool(name="const", bufs=1))
-        x_pool = ctx.enter_context(tc.tile_pool(name="x_pool", bufs=STEPS))
-        stage = ctx.enter_context(tc.tile_pool(name="stage", bufs=2))
+        x_pool = ctx.enter_context(tc.tile_pool(name="x_pool", bufs=TILES // PAIR))
+        stage = ctx.enter_context(tc.tile_pool(name="stage", bufs=2 * PAIR))
         results = ctx.enter_context(tc.tile_pool(name="results", bufs=3))
         psum_t = ctx.enter_context(tc.psum_pool(name="psum_t", bufs=PAIR))
         psum_o = ctx.enter_context(tc.psum_pool(name="psum_o", bufs=PAIR))
@@ -69,12 +67,18 @@ def tile_attention_pa_t_kernel(
 
         x_tiles = {}
 
-        def load_x(s):
-            b, i0 = divmod(s * PAIR, ROWS)
-            x_tiles[s] = x_pool.tile([P, PAIR, DIM], BF16, name="x_pair")
-            nc.sync.dma_start(out=x_tiles[s][:], in_=x_rows[b][:, i0 : i0 + PAIR, :])
+        def load_x(n, count):
+            first = n - n % PAIR
+            if n == first:
+                x_tiles[first] = x_pool.tile([P, PAIR, DIM], BF16, name="x_pair")
+            b, i0 = divmod(n, ROWS)
+            nc.sync.dma_start(
+                out=x_tiles[first][:, n - first : n - first + count, :],
+                in_=x_rows[b][:, i0 : i0 + count, :],
+            )
 
-        load_x(0)
+        load_x(0, 1)
+        load_x(1, 1)
         nc.sync.dma_start(
             out=w_words[:].bitcast(I32), in_=Wqkv_words.rearrange("g p n -> p g n").bitcast(I32)
         )
@@ -83,8 +87,8 @@ def tile_attention_pa_t_kernel(
             nc.sync.dma_start(
                 out=w_scales[r:P:32, :, :].bitcast(I32), in_=scale_rows[r].bitcast(I32)
             )
-        for s in range(1, STEPS):
-            load_x(s)
+        for n in range(PAIR, TILES, PAIR):
+            load_x(n, PAIR)
 
         def make_table(i_lo, i_hi):
             f_in = angles[:, :, i_lo:i_hi, :]
@@ -106,63 +110,58 @@ def tile_attention_pa_t_kernel(
 
         flipped, grouped, codes, x_scales, banks, rotated, v_rows = {}, {}, {}, {}, {}, {}, {}
 
-        def transpose(s):
-            for e in range(PAIR):
-                flipped[s, e] = psum_t.tile([P, PASSES, 2, P], F32, name="flipped")
-                words = x_tiles[s][:, e, :].bitcast(F32)
-                for g in range(PASSES):
-                    for u in range(2):
-                        nc.tensor.transpose(
-                            flipped[s, e][:, g, u, :],
-                            words[:, WORDS * g + u : WORDS * (g + 1) : 2],
-                            ident[:],
-                        )
+        def transpose(n):
+            flipped[n] = psum_t.tile([P, PASSES, 2, P], F32, name="flipped")
+            words = x_tiles[n - n % PAIR][:, n % PAIR, :].bitcast(F32)
+            for g in range(PASSES):
+                for u in range(2):
+                    nc.tensor.transpose(
+                        flipped[n][:, g, u, :],
+                        words[:, WORDS * g + u : WORDS * (g + 1) : 2],
+                        ident[:],
+                    )
 
-        def regroup(s):
-            grouped[s] = stage.tile(
-                [P, PAIR, PASSES, P, PACK], BF16, name="grouped", align_bytes=64
+        def regroup(n):
+            grouped[n] = stage.tile([P, PASSES, P, PACK], BF16, name="grouped", align_bytes=64)
+            nc.scalar.copy(
+                out=grouped[n][:].bitcast(F32),
+                in_=flipped[n][:].rearrange("p g u r -> p g r u"),
             )
-            for e in range(PAIR):
-                nc.scalar.copy(
-                    out=grouped[s][:, e].bitcast(F32),
-                    in_=flipped[s, e][:].rearrange("p g u r -> p g r u"),
-                )
 
-        def quantise(s):
-            codes[s] = stage.tile([P, PAIR * PASSES, P], U32, name="codes", align_bytes=64)
-            x_scales[s] = stage.tile([P, PAIR * PASSES, P], U8, name="x_scales", align_bytes=64)
+        def quantise(n):
+            codes[n] = stage.tile([P, PASSES, P], U32, name="codes", align_bytes=64)
+            x_scales[n] = stage.tile([P, PASSES, P], U8, name="x_scales", align_bytes=64)
             nc.vector.quantize_mx(
-                out=codes[s][:].rearrange("p c r -> p (c r)").bitcast(FP8X4),
-                scales=x_scales[s][:].rearrange("p c r -> p (c r)"),
-                in_=grouped[s][:].rearrange("p e g r t -> p (e g r t)"),
+                out=codes[n][:].rearrange("p g r -> p (g r)").bitcast(FP8X4),
+                scales=x_scales[n][:].rearrange("p g r -> p (g r)"),
+                in_=grouped[n][:].rearrange("p g r t -> p (g r t)"),
             )
 
-        def project(s, e):
+        def project(n):
             for part in range(3):
                 bank = psum_o.tile([P, PART], F32, name="bank%d" % part)
-                banks[s, e, part] = bank
+                banks[n, part] = bank
                 for c in range(PART // CHUNK):
                     col = part * PART + c * CHUNK
                     for g in range(PASSES):
                         nc.tensor.matmul_mx(
                             out=bank[:, c * CHUNK : (c + 1) * CHUNK],
-                            lhsT=codes[s][:, e * PASSES + g, :].bitcast(FP8X4),
-                            lhsT_scale=x_scales[s][:, e * PASSES + g, :],
+                            lhsT=codes[n][:, g, :].bitcast(FP8X4),
+                            lhsT_scale=x_scales[n][:, g, :],
                             rhs=w_words[:, g, 2 * col : 2 * (col + CHUNK)].bitcast(FP4X4),
                             rhs_scale=w_scales[:, g, col : col + CHUNK],
                             start=(g == 0),
                             stop=(g == PASSES - 1),
                         )
 
-        def rotate(s, e):
-            n = s * PAIR + e
+        def rotate(n):
             if n % GROUP == 0:
                 rotated[n // GROUP] = results.tile(
                     [P, 2, 2 * HEADS, GROUP, HEAD_DIM], F32, name="rotated"
                 )
             both = [P, 2, HEADS, HEAD_DIM]
             for part in range(2):
-                by_head = banks[s, e, part][:].rearrange("p (h d) -> p h d", h=HEADS)
+                by_head = banks[n, part][:].rearrange("p (h d) -> p h d", h=HEADS)
                 nc.vector.tensor_tensor(
                     out=rotated[n // GROUP][:, :, part * HEADS : (part + 1) * HEADS, n % GROUP, :],
                     in0=by_head.unsqueeze(1).to_broadcast(both),
@@ -170,18 +169,17 @@ def tile_attention_pa_t_kernel(
                     op=MULT,
                 )
 
-        def keep_v(s, e):
-            n = s * PAIR + e
+        def keep_v(n):
             if n % GROUP == 0:
                 v_rows[n // GROUP] = results.tile([P, HEADS, GROUP, HEAD_DIM], F32, name="v_rows")
             nc.scalar.copy(
                 out=v_rows[n // GROUP][:, :, n % GROUP, :],
-                in_=banks[s, e, 2][:].rearrange("p (h d) -> p h d", h=HEADS),
+                in_=banks[n, 2][:].rearrange("p (h d) -> p h d", h=HEADS),
             )
 
-        def add_up(engine, s):
-            m, lo = divmod(s * PAIR, GROUP)
-            halves = rotated[m][:, :, :, lo : lo + PAIR, :].rearrange(
+        def add_up(engine, n, count):
+            m, lo = divmod(n, GROUP)
+            halves = rotated[m][:, :, :, lo : lo + count, :].rearrange(
                 "p t c i (a f e) -> p t c (i a) f e", a=AXES, f=2
             )
             for f in range(2):
@@ -204,31 +202,43 @@ def tile_attention_pa_t_kernel(
                     in_=rotated[m][:, 0, part * HEADS : (part + 1) * HEADS, lo : lo + count, :],
                 )
 
-        transpose(0)
-        regroup(0)
-        quantise(0)
+        for n in range(PAIR):
+            transpose(n)
+            regroup(n)
+            quantise(n)
         make_table(0, GROUP)
-        for s in range(STEPS):
-            n = s * PAIR
-            project(s, 0)
-            if s == 0:
-                transpose(1)
-                regroup(1)
-            project(s, 1)
-            if s + 2 < STEPS:
-                transpose(s + 2)
-            rotate(s, 0)
-            if s + 1 < STEPS:
-                quantise(s + 1)
-            rotate(s, 1)
-            keep_v(s, 0)
-            keep_v(s, 1)
-            if s + 2 < STEPS:
-                regroup(s + 2)
+        for n in range(0, TILES, PAIR):
+            ahead = [t for t in (n + 2 * PAIR, n + 2 * PAIR + 1) if t < TILES]
+            coming = [t for t in (n + PAIR, n + PAIR + 1) if t < TILES]
+            last = n + PAIR == TILES
+            project(n)
+            if n == 0:
+                for t in coming:
+                    transpose(t)
+                    regroup(t)
+            project(n + 1)
+            for t in ahead:
+                transpose(t)
+            rotate(n)
+            if last:
+                add_up(nc.vector, n, 1)
+            for t in coming:
+                quantise(t)
+            rotate(n + 1)
+            if last:
+                add_up(nc.vector, n + 1, 1)
+            else:
+                add_up(nc.gpsimd, n, PAIR)
+            keep_v(n)
+            keep_v(n + 1)
+            for t in ahead:
+                regroup(t)
             if n % GROUP == 0 and n + GROUP < ROWS:
                 make_table(n + GROUP, n + 2 * GROUP)
-            add_up(nc.vector if s == STEPS - 1 else nc.gpsimd, s)
-            if n >= TILES - GROUP:
+            if last:
+                store(n, 1)
+                store(n + 1, 1)
+            elif n + GROUP >= TILES:
                 store(n, PAIR)
             elif (n + PAIR) % GROUP == 0:
                 store(n + PAIR - GROUP, GROUP)

@@ -28,6 +28,7 @@ ROWS = TOKENS // P
 TILES = BATCH * ROWS
 PAIR = 2
 GROUP = 4
+UNSORTED = 2 * PAIR
 
 FLOPS = 2 * BATCH * TOKENS * DIM * 3 * PART
 
@@ -43,6 +44,7 @@ def tile_attention_pa_t_kernel(
         const = ctx.enter_context(tc.tile_pool(name="const", bufs=1))
         x_pool = ctx.enter_context(tc.tile_pool(name="x_pool", bufs=TILES // PAIR))
         stage = ctx.enter_context(tc.tile_pool(name="stage", bufs=2 * PAIR))
+        sorting = ctx.enter_context(tc.tile_pool(name="sorting", bufs=2))
         results = ctx.enter_context(tc.tile_pool(name="results", bufs=3))
         psum_t = ctx.enter_context(tc.psum_pool(name="psum_t", bufs=PAIR))
         psum_o = ctx.enter_context(tc.psum_pool(name="psum_o", bufs=PAIR))
@@ -77,16 +79,16 @@ def tile_attention_pa_t_kernel(
                 in_=x_rows[b][:, i0 : i0 + count, :],
             )
 
-        load_x(0, 1)
-        load_x(1, 1)
-        nc.sync.dma_start(
-            out=w_words[:].bitcast(I32), in_=Wqkv_words.rearrange("g p n -> p g n").bitcast(I32)
-        )
         scale_rows = Wqkv_scales.rearrange("g (q r) n -> r q g n", r=4)
         for r in range(4):
             nc.sync.dma_start(
                 out=w_scales[r:P:32, :, :].bitcast(I32), in_=scale_rows[r].bitcast(I32)
             )
+        load_x(0, 1)
+        load_x(1, 1)
+        nc.sync.dma_start(
+            out=w_words[:].bitcast(I32), in_=Wqkv_words.rearrange("g p n -> p g n").bitcast(I32)
+        )
         for n in range(PAIR, TILES, PAIR):
             load_x(n, PAIR)
 
@@ -108,18 +110,28 @@ def tile_attention_pa_t_kernel(
                 out=s_halves[:, :, :, 1, :], in_=f_halves[:, :, :, 0, :], func=SIN, scale=-1.0
             )
 
-        flipped, grouped, codes, x_scales, banks, rotated, v_rows = {}, {}, {}, {}, {}, {}, {}
+        ordered, flipped, grouped, codes, x_scales = {}, {}, {}, {}, {}
+        banks, rotated, v_rows = {}, {}, {}
+
+        def sort_words(n):
+            ordered[n] = sorting.tile([P, PAIR, PASSES, 2, P], F32, name="ordered")
+            nc.scalar.copy(
+                out=ordered[n][:].rearrange("p e g u q -> p (e g) u q"),
+                in_=x_tiles[n][:]
+                .bitcast(F32)
+                .rearrange("p e (g q u) -> p (e g) u q", g=PASSES, u=2),
+            )
 
         def transpose(n):
             flipped[n] = psum_t.tile([P, PASSES, 2, P], F32, name="flipped")
             words = x_tiles[n - n % PAIR][:, n % PAIR, :].bitcast(F32)
             for g in range(PASSES):
                 for u in range(2):
-                    nc.tensor.transpose(
-                        flipped[n][:, g, u, :],
-                        words[:, WORDS * g + u : WORDS * (g + 1) : 2],
-                        ident[:],
-                    )
+                    if n < UNSORTED:
+                        columns = words[:, WORDS * g + u : WORDS * (g + 1) : 2]
+                    else:
+                        columns = ordered[n - n % PAIR][:, n % PAIR, g, u, :]
+                    nc.tensor.transpose(flipped[n][:, g, u, :], columns, ident[:])
 
         def regroup(n):
             grouped[n] = stage.tile([P, PASSES, P, PACK], BF16, name="grouped", align_bytes=64)
@@ -207,6 +219,7 @@ def tile_attention_pa_t_kernel(
             regroup(n)
             quantise(n)
         make_table(0, GROUP)
+        sort_words(UNSORTED)
         for n in range(0, TILES, PAIR):
             ahead = [t for t in (n + 2 * PAIR, n + 2 * PAIR + 1) if t < TILES]
             coming = [t for t in (n + PAIR, n + PAIR + 1) if t < TILES]
@@ -220,25 +233,19 @@ def tile_attention_pa_t_kernel(
             for t in ahead:
                 transpose(t)
             rotate(n)
-            if last:
-                add_up(nc.vector, n, 1)
             for t in coming:
                 quantise(t)
             rotate(n + 1)
-            if last:
-                add_up(nc.vector, n + 1, 1)
-            else:
-                add_up(nc.gpsimd, n, PAIR)
+            add_up(nc.vector if last else nc.gpsimd, n, PAIR)
             keep_v(n)
             keep_v(n + 1)
             for t in ahead:
                 regroup(t)
+            if n + 3 * PAIR < TILES:
+                sort_words(n + 3 * PAIR)
             if n % GROUP == 0 and n + GROUP < ROWS:
                 make_table(n + GROUP, n + 2 * GROUP)
-            if last:
-                store(n, 1)
-                store(n + 1, 1)
-            elif n + GROUP >= TILES:
+            if n + GROUP >= TILES:
                 store(n, PAIR)
             elif (n + PAIR) % GROUP == 0:
                 store(n + PAIR - GROUP, GROUP)

@@ -43,7 +43,7 @@ def tile_attention_pa_t_kernel(
     with ExitStack() as ctx:
         const = ctx.enter_context(tc.tile_pool(name="const", bufs=1))
         x_pool = ctx.enter_context(tc.tile_pool(name="x_pool", bufs=TILES // PAIR))
-        stage = ctx.enter_context(tc.tile_pool(name="stage", bufs=2 * PAIR))
+        stage = ctx.enter_context(tc.tile_pool(name="stage", bufs=3))
         sorting = ctx.enter_context(tc.tile_pool(name="sorting", bufs=2))
         results = ctx.enter_context(tc.tile_pool(name="results", bufs=3))
         psum_t = ctx.enter_context(tc.psum_pool(name="psum_t", bufs=PAIR))
@@ -134,19 +134,28 @@ def tile_attention_pa_t_kernel(
                     nc.tensor.transpose(flipped[n][:, g, u, :], columns, ident[:])
 
         def regroup(n):
-            grouped[n] = stage.tile([P, PASSES, P, PACK], BF16, name="grouped", align_bytes=64)
+            first = n - n % PAIR
+            if n == first:
+                grouped[first] = stage.tile(
+                    [P, PAIR, PASSES, P, PACK], BF16, name="grouped", align_bytes=64
+                )
             nc.scalar.copy(
-                out=grouped[n][:].bitcast(F32),
+                out=grouped[first][:, n - first, :, :, :].bitcast(F32),
                 in_=flipped[n][:].rearrange("p g u r -> p g r u"),
             )
 
-        def quantise(n):
-            codes[n] = stage.tile([P, PASSES, P], U32, name="codes", align_bytes=64)
-            x_scales[n] = stage.tile([P, PASSES, P], U8, name="x_scales", align_bytes=64)
+        def quantise(n, count):
+            first = n - n % PAIR
+            if n == first:
+                codes[first] = stage.tile([P, PAIR, PASSES, P], U32, name="codes", align_bytes=64)
+                x_scales[first] = stage.tile(
+                    [P, PAIR, PASSES, P], U8, name="x_scales", align_bytes=64
+                )
+            lo, hi = n - first, n - first + count
             nc.vector.quantize_mx(
-                out=codes[n][:].rearrange("p g r -> p (g r)").bitcast(FP8X4),
-                scales=x_scales[n][:].rearrange("p g r -> p (g r)"),
-                in_=grouped[n][:].rearrange("p g r t -> p (g r t)"),
+                out=codes[first][:, lo:hi, :, :].rearrange("p e g r -> p (e g r)").bitcast(FP8X4),
+                scales=x_scales[first][:, lo:hi, :, :].rearrange("p e g r -> p (e g r)"),
+                in_=grouped[first][:, lo:hi, :, :, :].rearrange("p e g r t -> p (e g r t)"),
             )
 
         def project(n):
@@ -158,8 +167,8 @@ def tile_attention_pa_t_kernel(
                     for g in range(PASSES):
                         nc.tensor.matmul_mx(
                             out=bank[:, c * CHUNK : (c + 1) * CHUNK],
-                            lhsT=codes[n][:, g, :].bitcast(FP8X4),
-                            lhsT_scale=x_scales[n][:, g, :],
+                            lhsT=codes[n - n % PAIR][:, n % PAIR, g, :].bitcast(FP8X4),
+                            lhsT_scale=x_scales[n - n % PAIR][:, n % PAIR, g, :],
                             rhs=w_words[:, g, 2 * col : 2 * (col + CHUNK)].bitcast(FP4X4),
                             rhs_scale=w_scales[:, g, col : col + CHUNK],
                             start=(g == 0),
@@ -217,7 +226,7 @@ def tile_attention_pa_t_kernel(
         for n in range(PAIR):
             transpose(n)
             regroup(n)
-            quantise(n)
+            quantise(n, 1)
         make_table(0, GROUP)
         sort_words(UNSORTED)
         for n in range(0, TILES, PAIR):
@@ -232,9 +241,12 @@ def tile_attention_pa_t_kernel(
             project(n + 1)
             for t in ahead:
                 transpose(t)
-            rotate(n)
-            for t in coming:
-                quantise(t)
+            if n == 0:
+                rotate(n)
+            if coming:
+                quantise(coming[0], PAIR)
+            if n > 0:
+                rotate(n)
             rotate(n + 1)
             add_up(nc.vector if last else nc.gpsimd, n, PAIR)
             keep_v(n)

@@ -29,6 +29,8 @@ TILES = BATCH * ROWS
 PAIR = 2
 GROUP = 4
 UNSORTED = 2 * PAIR
+HALF = AXIS_DIM // 2
+BLOCK = 2 * PART
 
 FLOPS = 2 * BATCH * TOKENS * DIM * 3 * PART
 
@@ -46,6 +48,7 @@ def tile_attention_pa_t_kernel(
         stage = ctx.enter_context(tc.tile_pool(name="stage", bufs=3))
         sorting = ctx.enter_context(tc.tile_pool(name="sorting", bufs=2))
         results = ctx.enter_context(tc.tile_pool(name="results", bufs=3))
+        factors = ctx.enter_context(tc.tile_pool(name="factors", bufs=3))
         psum_t = ctx.enter_context(tc.psum_pool(name="psum_t", bufs=PAIR))
         psum_o = ctx.enter_context(tc.psum_pool(name="psum_o", bufs=PAIR))
         ctx.enter_context(tc.manual_schedule())
@@ -61,7 +64,7 @@ def tile_attention_pa_t_kernel(
         w_scales = const.tile([P, PASSES, 3 * PART], U8, name="w_scales", align_bytes=64)
         nc.vector.memset(w_scales[:].bitcast(I32), 0)
         w_words = const.tile([P, PASSES, 2 * 3 * PART], U8, name="w_words", align_bytes=64)
-        table = const.tile([P, ROWS, 2, HEAD_DIM], F32, name="table")
+        table = const.tile([P, ROWS, 2, 2, AXES * HALF], F32, name="table")
 
         zero = const.tile([P, 1], F32, name="zero")
         nc.vector.memset(zero[:], 0.0)
@@ -93,25 +96,25 @@ def tile_attention_pa_t_kernel(
             load_x(n, PAIR)
 
         def make_table(i_lo, i_hi):
-            f_in = angles[:, :, i_lo:i_hi, :]
-            nc.scalar.activation(
-                out=table[:, i_lo:i_hi, 0, :].rearrange("p i (a e) -> p i a e", a=AXES),
-                in_=f_in.rearrange("p a i e -> p i a e"),
-                func=SIN,
-                bias=math.pi / 2,
-                scale=-1.0,
-            )
-            f_halves = f_in.rearrange("p a i (f e) -> p i a f e", f=2)
-            s_halves = table[:, i_lo:i_hi, 1, :].rearrange("p i (a f e) -> p i a f e", a=AXES, f=2)
-            nc.scalar.activation(
-                out=s_halves[:, :, :, 0, :], in_=f_halves[:, :, :, 1, :], func=SIN, scale=1.0
-            )
-            nc.scalar.activation(
-                out=s_halves[:, :, :, 1, :], in_=f_halves[:, :, :, 0, :], func=SIN, scale=-1.0
-            )
+            for f in range(2):
+                own = angles[:, :, i_lo:i_hi, f * HALF : (f + 1) * HALF]
+                other = angles[:, :, i_lo:i_hi, (1 - f) * HALF : (2 - f) * HALF]
+                nc.scalar.activation(
+                    out=table[:, i_lo:i_hi, f, 0, :].rearrange("p i (a e) -> p i a e", a=AXES),
+                    in_=own.rearrange("p a i e -> p i a e"),
+                    func=SIN,
+                    bias=math.pi / 2,
+                    scale=-1.0,
+                )
+                nc.scalar.activation(
+                    out=table[:, i_lo:i_hi, f, 1, :].rearrange("p i (a e) -> p i a e", a=AXES),
+                    in_=other.rearrange("p a i e -> p i a e"),
+                    func=SIN,
+                    scale=1.0 - 2.0 * f,
+                )
 
         ordered, flipped, grouped, codes, x_scales = {}, {}, {}, {}, {}
-        banks, rotated, v_rows = {}, {}, {}
+        banks, products, rotated, v_rows = {}, {}, {}, {}
 
         def sort_words(n):
             ordered[n] = sorting.tile([P, PAIR, PASSES, 2, P], F32, name="ordered")
@@ -176,19 +179,29 @@ def tile_attention_pa_t_kernel(
                         )
 
         def rotate(n):
-            if n % GROUP == 0:
-                rotated[n // GROUP] = results.tile(
-                    [P, 2, 2 * HEADS, GROUP, HEAD_DIM], F32, name="rotated"
-                )
-            both = [P, 2, HEADS, HEAD_DIM]
+            first = n - n % PAIR
+            if n == first:
+                products[first] = factors.tile([P, 2 * PAIR * BLOCK + AXIS_DIM], F32, name="products")
+            shape = [P, 2, HEADS, AXES, HALF]
             for part in range(2):
-                by_head = banks[n, part][:].rearrange("p (h d) -> p h d", h=HEADS)
-                nc.vector.tensor_tensor(
-                    out=rotated[n // GROUP][:, :, part * HEADS : (part + 1) * HEADS, n % GROUP, :],
-                    in0=by_head.unsqueeze(1).to_broadcast(both),
-                    in1=table[:, n % ROWS, :, :].unsqueeze(2).to_broadcast(both),
-                    op=MULT,
-                )
+                start = ((n - first) * 2 + part) * BLOCK
+                for f in range(2):
+                    step = PART + (1 - 2 * f) * HALF
+                    lo = start + f * HALF
+                    nc.vector.tensor_tensor(
+                        out=products[first][:, lo : lo + 2 * step]
+                        .rearrange("p (u k e) -> p u k e", u=2, e=HALF)[:, :, 0 : 2 * HEADS * AXES - 1 : 2, :]
+                        .rearrange("p u (h a) e -> p u h a e", h=HEADS),
+                        in0=banks[n, part][:]
+                        .rearrange("p (h a f e) -> p h a f e", h=HEADS, a=AXES, f=2)[:, :, :, f, :]
+                        .unsqueeze(1)
+                        .to_broadcast(shape),
+                        in1=table[:, n % ROWS, f, :, :]
+                        .rearrange("p u (a e) -> p u a e", a=AXES)
+                        .unsqueeze(2)
+                        .to_broadcast(shape),
+                        op=MULT,
+                    )
 
         def keep_v(n):
             if n % GROUP == 0:
@@ -198,18 +211,19 @@ def tile_attention_pa_t_kernel(
                 in_=banks[n, 2][:].rearrange("p (h d) -> p h d", h=HEADS),
             )
 
-        def add_up(engine, n, count):
+        def add_up(engine, n):
             m, lo = divmod(n, GROUP)
-            halves = rotated[m][:, :, :, lo : lo + count, :].rearrange(
-                "p t c i (a f e) -> p t c (i a) f e", a=AXES, f=2
+            if lo == 0:
+                rotated[m] = results.tile([P, 2 * HEADS, GROUP, HEAD_DIM], F32, name="rotated")
+            both = products[n][:, 0 : 2 * PAIR * BLOCK].rearrange(
+                "p (i b t h d) -> p t i b h d", i=PAIR, b=2, t=2, h=HEADS
             )
-            for f in range(2):
-                engine.tensor_tensor(
-                    out=halves[:, 0, :, :, f, :],
-                    in0=halves[:, 0, :, :, f, :],
-                    in1=halves[:, 1, :, :, 1 - f, :],
-                    op=ADD,
-                )
+            engine.tensor_tensor(
+                out=rotated[m][:, :, lo : lo + PAIR, :].rearrange("p (b h) i d -> p i b h d", b=2),
+                in0=both[:, 0, :, :, :, :],
+                in1=both[:, 1, :, :, :, :],
+                op=ADD,
+            )
 
         def store(n, count):
             m, lo = divmod(n, GROUP)
@@ -220,7 +234,7 @@ def tile_attention_pa_t_kernel(
             for part in range(2):
                 nc.sync.dma_start(
                     out=out_rows[part][b][:, :, i0 : i0 + count, :],
-                    in_=rotated[m][:, 0, part * HEADS : (part + 1) * HEADS, lo : lo + count, :],
+                    in_=rotated[m][:, part * HEADS : (part + 1) * HEADS, lo : lo + count, :],
                 )
 
         for n in range(PAIR):
@@ -248,7 +262,7 @@ def tile_attention_pa_t_kernel(
             if n > 0:
                 rotate(n)
             rotate(n + 1)
-            add_up(nc.vector if last else nc.gpsimd, n, PAIR)
+            add_up(nc.vector if last else nc.gpsimd, n)
             keep_v(n)
             keep_v(n + 1)
             for t in ahead:

@@ -53,13 +53,13 @@ def tile_attention_pa_t_kernel(
         psum_o = ctx.enter_context(tc.psum_pool(name="psum_o", bufs=PAIR))
         ctx.enter_context(tc.manual_schedule())
 
-        angles = const.tile([P, AXES, ROWS, AXIS_DIM], BF16, name="angles")
-        for a, f in enumerate((f1, f2, f3)):
-            nc.gpsimd.dma_start(
-                out=angles[:, a, :, :], in_=f.rearrange("(p i) e -> p i e", i=ROWS)
-            )
         ident = const.tile([P, P], F32, name="ident")
         make_identity(nc, ident[:])
+        angles = const.tile([P, AXES, ROWS, AXIS_DIM], BF16, name="angles")
+        for a, f in enumerate((f1, f2, f3)):
+            nc.scalar.dma_start(
+                out=angles[:, a, :, :], in_=f.rearrange("(p i) e -> p i e", i=ROWS)
+            )
 
         w_scales = const.tile([P, PASSES, 3 * PART], U8, name="w_scales", align_bytes=64)
         nc.vector.memset(w_scales[:].bitcast(I32), 0)

@@ -211,31 +211,33 @@ def tile_attention_pa_t_kernel(
                 in_=banks[n, 2][:].rearrange("p (h d) -> p h d", h=HEADS),
             )
 
-        def add_up(engine, n):
+        def add_up(engine, n, count, parts):
+            first = n - n % PAIR
             m, lo = divmod(n, GROUP)
             if lo == 0:
                 rotated[m] = results.tile([P, 2 * HEADS, GROUP, HEAD_DIM], F32, name="rotated")
-            both = products[n][:, 0 : 2 * PAIR * BLOCK].rearrange(
+            both = products[first][:, 0 : 2 * PAIR * BLOCK].rearrange(
                 "p (i b t h d) -> p t i b h d", i=PAIR, b=2, t=2, h=HEADS
-            )
+            )[:, :, n - first : n - first + count, parts, :, :]
             engine.tensor_tensor(
-                out=rotated[m][:, :, lo : lo + PAIR, :].rearrange("p (b h) i d -> p i b h d", b=2),
+                out=rotated[m][:, :, lo : lo + count, :].rearrange("p (b h) i d -> p i b h d", b=2)[
+                    :, :, parts, :, :
+                ],
                 in0=both[:, 0, :, :, :, :],
                 in1=both[:, 1, :, :, :, :],
                 op=ADD,
             )
 
-        def store(n, count):
+        def store(n, count, parts):
             m, lo = divmod(n, GROUP)
             b, i0 = divmod(n, ROWS)
-            nc.sync.dma_start(
-                out=out_rows[2][b][:, :, i0 : i0 + count, :], in_=v_rows[m][:, :, lo : lo + count, :]
-            )
-            for part in range(2):
-                nc.sync.dma_start(
-                    out=out_rows[part][b][:, :, i0 : i0 + count, :],
-                    in_=rotated[m][:, part * HEADS : (part + 1) * HEADS, lo : lo + count, :],
-                )
+            for part in parts:
+                if part == 2:
+                    rows = v_rows[m][:, :, lo : lo + count, :]
+                else:
+                    rows = rotated[m][:, part * HEADS : (part + 1) * HEADS, lo : lo + count, :]
+                queue = nc.scalar if part == 2 else nc.sync
+                queue.dma_start(out=out_rows[part][b][:, :, i0 : i0 + count, :], in_=rows)
 
         for n in range(PAIR):
             transpose(n)
@@ -262,9 +264,17 @@ def tile_attention_pa_t_kernel(
             if n > 0:
                 rotate(n)
             rotate(n + 1)
-            add_up(nc.vector if last else nc.gpsimd, n)
+            if last:
+                add_up(nc.vector, n, PAIR, slice(0, 1))
+                add_up(nc.vector, n, PAIR, slice(1, 2))
+            else:
+                add_up(nc.gpsimd, n, PAIR, slice(0, 2))
             keep_v(n)
             keep_v(n + 1)
+            if n + GROUP >= TILES:
+                store(n, PAIR, (2,))
+            elif (n + PAIR) % GROUP == 0:
+                store(n + PAIR - GROUP, GROUP, (2,))
             for t in ahead:
                 regroup(t)
             if n + 3 * PAIR < TILES:
@@ -272,6 +282,6 @@ def tile_attention_pa_t_kernel(
             if n % GROUP == 0 and n + GROUP < ROWS:
                 make_table(n + GROUP, n + 2 * GROUP)
             if n + GROUP >= TILES:
-                store(n, PAIR)
+                store(n, PAIR, (0, 1))
             elif (n + PAIR) % GROUP == 0:
-                store(n + PAIR - GROUP, GROUP)
+                store(n + PAIR - GROUP, GROUP, (0, 1))

@@ -31,6 +31,7 @@ GROUP = 4
 UNSORTED = 2 * PAIR
 HALF = AXIS_DIM // 2
 BLOCK = 2 * PART
+WARM_UP = 7
 
 FLOPS = 2 * BATCH * TOKENS * DIM * 3 * PART
 
@@ -69,6 +70,18 @@ def tile_attention_pa_t_kernel(
         zero = const.tile([P, 1], F32, name="zero")
         nc.vector.memset(zero[:], 0.0)
         nc.scalar.activation(out=zero[:], in_=zero[:], func=SIN)
+
+        cold = const.tile([P, 4 * P], BF16, name="cold")
+        nc.vector.memset(cold[:], 0.0)
+        warmth = psum_t.tile([P, PASSES, 2, P], F32, name="flipped")
+        for turn in range(WARM_UP):
+            nc.tensor.matmul(
+                out=warmth[:].rearrange("p g u r -> p (g u r)"),
+                lhsT=cold[:, 0:P],
+                rhs=cold[:],
+                start=True,
+                stop=True,
+            )
 
         x_tiles = {}
 

@@ -32,6 +32,7 @@ UNSORTED = 2 * PAIR
 HALF = AXIS_DIM // 2
 BLOCK = 2 * PART
 WARM_UP = 7
+KEEP_WARM = 3
 
 FLOPS = 2 * BATCH * TOKENS * DIM * 3 * PART
 
@@ -256,6 +257,9 @@ def tile_attention_pa_t_kernel(
             transpose(n)
             regroup(n)
             quantise(n, 1)
+        idle = psum_o.tile([P, PART], F32, name="bank2")
+        for turn in range(KEEP_WARM):
+            nc.tensor.matmul(out=idle[:], lhsT=cold[:, 0:P], rhs=cold[:, 0:PART], start=True, stop=True)
         make_table(0, GROUP)
         sort_words(UNSORTED)
         for n in range(0, TILES, PAIR):

@@ -28,10 +28,10 @@ ROWS = TOKENS // P
 TILES = BATCH * ROWS
 PAIR = 2
 GROUP = 4
-UNSORTED = 2 * PAIR
+UNSORTED = 3 * PAIR
 HALF = AXIS_DIM // 2
 BLOCK = 2 * PART
-WARM_UP = 7
+WARM_UP = 16
 KEEP_WARM = 3
 
 FLOPS = 2 * BATCH * TOKENS * DIM * 3 * PART
@@ -58,10 +58,8 @@ def tile_attention_pa_t_kernel(
         ident = const.tile([P, P], F32, name="ident")
         make_identity(nc, ident[:])
         angles = const.tile([P, AXES, ROWS, AXIS_DIM], BF16, name="angles")
-        for a, f in enumerate((f1, f2, f3)):
-            nc.scalar.dma_start(
-                out=angles[:, a, :, :], in_=f.rearrange("(p i) e -> p i e", i=ROWS)
-            )
+        cold = const.tile([P, P], BF16, name="cold")
+        nc.vector.memset(cold[:], 0.0)
 
         w_scales = const.tile([P, PASSES, 3 * PART], U8, name="w_scales", align_bytes=64)
         nc.vector.memset(w_scales[:].bitcast(I32), 0)
@@ -72,13 +70,11 @@ def tile_attention_pa_t_kernel(
         nc.vector.memset(zero[:], 0.0)
         nc.scalar.activation(out=zero[:], in_=zero[:], func=SIN)
 
-        cold = const.tile([P, 4 * P], BF16, name="cold")
-        nc.vector.memset(cold[:], 0.0)
         warmth = psum_t.tile([P, PASSES, 2, P], F32, name="flipped")
         for turn in range(WARM_UP):
             nc.tensor.matmul(
-                out=warmth[:].rearrange("p g u r -> p (g u r)"),
-                lhsT=cold[:, 0:P],
+                out=warmth[:, 0, 0, :],
+                lhsT=cold[:],
                 rhs=cold[:],
                 start=True,
                 stop=True,
@@ -96,16 +92,20 @@ def tile_attention_pa_t_kernel(
                 in_=x_rows[b][:, i0 : i0 + count, :],
             )
 
+        load_x(0, 1)
+        load_x(1, 1)
         scale_rows = Wqkv_scales.rearrange("g (q r) n -> r q g n", r=4)
         for r in range(4):
             nc.sync.dma_start(
                 out=w_scales[r:P:32, :, :].bitcast(I32), in_=scale_rows[r].bitcast(I32)
             )
-        load_x(0, 1)
-        load_x(1, 1)
         nc.sync.dma_start(
             out=w_words[:].bitcast(I32), in_=Wqkv_words.rearrange("g p n -> p g n").bitcast(I32)
         )
+        for a, f in enumerate((f1, f2, f3)):
+            nc.sync.dma_start(
+                out=angles[:, a, :, :], in_=f.rearrange("(p i) e -> p i e", i=ROWS)
+            )
         for n in range(PAIR, TILES, PAIR):
             load_x(n, PAIR)
 
@@ -192,13 +192,13 @@ def tile_attention_pa_t_kernel(
                             stop=(g == PASSES - 1),
                         )
 
-        def rotate(n):
+        def rotate(n, parts):
             first = n - n % PAIR
-            if n == first:
+            if first not in products:
                 products[first] = factors.tile([P, 2 * PAIR * BLOCK + AXIS_DIM], F32, name="products")
             shape = [P, 2, HEADS, AXES, HALF]
-            for part in range(2):
-                start = ((n - first) * 2 + part) * BLOCK
+            for part in parts:
+                start = (part * PAIR + n - first) * BLOCK
                 for f in range(2):
                     step = PART + (1 - 2 * f) * HALF
                     lo = start + f * HALF
@@ -228,10 +228,10 @@ def tile_attention_pa_t_kernel(
         def add_up(engine, n, count, parts):
             first = n - n % PAIR
             m, lo = divmod(n, GROUP)
-            if lo == 0:
+            if m not in rotated:
                 rotated[m] = results.tile([P, 2 * HEADS, GROUP, HEAD_DIM], F32, name="rotated")
             both = products[first][:, 0 : 2 * PAIR * BLOCK].rearrange(
-                "p (i b t h d) -> p t i b h d", i=PAIR, b=2, t=2, h=HEADS
+                "p (b i t h d) -> p t i b h d", b=2, i=PAIR, t=2, h=HEADS
             )[:, :, n - first : n - first + count, parts, :, :]
             engine.tensor_tensor(
                 out=rotated[m][:, :, lo : lo + count, :].rearrange("p (b h) i d -> p i b h d", b=2)[
@@ -259,36 +259,48 @@ def tile_attention_pa_t_kernel(
             quantise(n, 1)
         idle = psum_o.tile([P, PART], F32, name="bank2")
         for turn in range(KEEP_WARM):
-            nc.tensor.matmul(out=idle[:], lhsT=cold[:, 0:P], rhs=cold[:, 0:PART], start=True, stop=True)
-        make_table(0, GROUP)
-        sort_words(UNSORTED)
+            nc.tensor.matmul(out=idle[:, 0:P], lhsT=cold[:], rhs=cold[:], start=True, stop=True)
+        make_table(0, PAIR)
+        make_table(PAIR, GROUP)
         for n in range(0, TILES, PAIR):
-            ahead = [t for t in (n + 2 * PAIR, n + 2 * PAIR + 1) if t < TILES]
             coming = [t for t in (n + PAIR, n + PAIR + 1) if t < TILES]
+            ahead = [t for t in (n + 2 * PAIR, n + 2 * PAIR + 1) if t < TILES]
             last = n + PAIR == TILES
             project(n)
+            keep_v(n)
+            project(n + 1)
+            keep_v(n + 1)
             if n == 0:
                 for t in coming:
                     transpose(t)
                     regroup(t)
-            project(n + 1)
             for t in ahead:
                 transpose(t)
-            if n == 0:
-                rotate(n)
-            if coming:
+            if n > PAIR and coming:
                 quantise(coming[0], PAIR)
-            if n > 0:
-                rotate(n)
-            rotate(n + 1)
-            if last:
-                add_up(nc.vector, n, PAIR, slice(0, 1))
-                add_up(nc.vector, n, PAIR, slice(1, 2))
-            else:
+            if n == 0:
+                rotate(n, (0, 1))
+                rotate(n + 1, (0,))
+                quantise(coming[0], 1)
+                rotate(n + 1, (1,))
+                quantise(coming[1], 1)
                 add_up(nc.gpsimd, n, PAIR, slice(0, 2))
-            keep_v(n)
-            keep_v(n + 1)
-            if n + GROUP >= TILES:
+            elif last:
+                for part in range(2):
+                    for t in (n, n + 1):
+                        rotate(t, (part,))
+                    add_up((nc.gpsimd, nc.vector)[part], n, PAIR, slice(part, part + 1))
+            else:
+                rotate(n, (0, 1))
+                if n == PAIR:
+                    quantise(coming[0], PAIR)
+                rotate(n + 1, (0, 1))
+                if n + 2 * PAIR == TILES:
+                    add_up(nc.vector, n, PAIR, slice(1, 2))
+                    add_up(nc.gpsimd, n, PAIR, slice(0, 1))
+                else:
+                    add_up(nc.gpsimd, n, PAIR, slice(0, 2))
+            if n + 2 * GROUP >= TILES:
                 store(n, PAIR, (2,))
             elif (n + PAIR) % GROUP == 0:
                 store(n + PAIR - GROUP, GROUP, (2,))
@@ -296,9 +308,11 @@ def tile_attention_pa_t_kernel(
                 regroup(t)
             if n + 3 * PAIR < TILES:
                 sort_words(n + 3 * PAIR)
-            if n % GROUP == 0 and n + GROUP < ROWS:
-                make_table(n + GROUP, n + 2 * GROUP)
-            if n + GROUP >= TILES:
+            if n + GROUP < ROWS:
+                make_table(n + GROUP, n + GROUP + PAIR)
+            if n + 2 * PAIR == TILES:
+                store(n, PAIR, (1, 0))
+            elif n + 2 * GROUP >= TILES:
                 store(n, PAIR, (0, 1))
             elif (n + PAIR) % GROUP == 0:
                 store(n + PAIR - GROUP, GROUP, (0, 1))

@@ -32,7 +32,7 @@ UNSORTED = 3 * PAIR
 HALF = AXIS_DIM // 2
 BLOCK = 2 * PART
 WARM_UP = 16
-KEEP_WARM = 3
+KEEP_WARM = 6
 
 FLOPS = 2 * BATCH * TOKENS * DIM * 3 * PART
 
@@ -253,13 +253,13 @@ def tile_attention_pa_t_kernel(
                 queue = nc.scalar if part == 2 else nc.sync
                 queue.dma_start(out=out_rows[part][b][:, :, i0 : i0 + count, :], in_=rows)
 
+        idle = psum_o.tile([P, PART], F32, name="bank2")
         for n in range(PAIR):
             transpose(n)
+            for turn in range(KEEP_WARM):
+                nc.tensor.matmul(out=idle[:, 0:P], lhsT=cold[:], rhs=cold[:], start=True, stop=True)
             regroup(n)
             quantise(n, 1)
-        idle = psum_o.tile([P, PART], F32, name="bank2")
-        for turn in range(KEEP_WARM):
-            nc.tensor.matmul(out=idle[:, 0:P], lhsT=cold[:], rhs=cold[:], start=True, stop=True)
         make_table(0, PAIR)
         make_table(PAIR, GROUP)
         for n in range(0, TILES, PAIR):

@@ -106,7 +106,9 @@ def tile_attention_pa_t_kernel(
             nc.sync.dma_start(
                 out=angles[:, a, :, :], in_=f.rearrange("(p i) e -> p i e", i=ROWS)
             )
-        for n in range(PAIR, TILES, PAIR):
+        load_x(PAIR, 1)
+        load_x(PAIR + 1, 1)
+        for n in range(2 * PAIR, TILES, PAIR):
             load_x(n, PAIR)
 
         def make_table(i_lo, i_hi):
@@ -250,7 +252,7 @@ def tile_attention_pa_t_kernel(
                     rows = v_rows[m][:, :, lo : lo + count, :]
                 else:
                     rows = rotated[m][:, part * HEADS : (part + 1) * HEADS, lo : lo + count, :]
-                queue = nc.scalar if part == 2 else nc.sync
+                queue = nc.scalar if part == 2 and n + 2 * GROUP >= TILES else nc.sync
                 queue.dma_start(out=out_rows[part][b][:, :, i0 : i0 + count, :], in_=rows)
 
         idle = psum_o.tile([P, PART], F32, name="bank2")
@@ -268,21 +270,20 @@ def tile_attention_pa_t_kernel(
             last = n + PAIR == TILES
             project(n)
             keep_v(n)
-            project(n + 1)
-            keep_v(n + 1)
             if n == 0:
                 for t in coming:
                     transpose(t)
                     regroup(t)
+            project(n + 1)
+            keep_v(n + 1)
             for t in ahead:
                 transpose(t)
             if n > PAIR and coming:
                 quantise(coming[0], PAIR)
             if n == 0:
                 rotate(n, (0, 1))
-                rotate(n + 1, (0,))
                 quantise(coming[0], 1)
-                rotate(n + 1, (1,))
+                rotate(n + 1, (0, 1))
                 quantise(coming[1], 1)
                 add_up(nc.gpsimd, n, PAIR, slice(0, 2))
             elif last:

@@ -30,7 +30,6 @@ PAIR = 2
 GROUP = 4
 UNSORTED = 3 * PAIR
 HALF = AXIS_DIM // 2
-BLOCK = 2 * PART
 WARM_UP = 16
 KEEP_WARM = 6
 
@@ -64,7 +63,7 @@ def tile_attention_pa_t_kernel(
         w_scales = const.tile([P, PASSES, 3 * PART], U8, name="w_scales", align_bytes=64)
         nc.vector.memset(w_scales[:].bitcast(I32), 0)
         w_words = const.tile([P, PASSES, 2 * 3 * PART], U8, name="w_words", align_bytes=64)
-        table = const.tile([P, ROWS, 2, 2, AXES * HALF], F32, name="table")
+        table = const.tile([P, ROWS, 2, HEAD_DIM], F32, name="table")
 
         zero = const.tile([P, 1], F32, name="zero")
         nc.vector.memset(zero[:], 0.0)
@@ -112,19 +111,15 @@ def tile_attention_pa_t_kernel(
             load_x(n, PAIR)
 
         def make_table(i_lo, i_hi):
+            own = angles[:, :, i_lo:i_hi, :].rearrange("p a i e -> p i a e")
+            rows = table[:, i_lo:i_hi, :, :].rearrange("p i u (a e) -> p i u a e", a=AXES)
+            nc.scalar.activation(
+                out=rows[:, :, 0, :, :], in_=own, func=SIN, bias=math.pi / 2, scale=-1.0
+            )
             for f in range(2):
-                own = angles[:, :, i_lo:i_hi, f * HALF : (f + 1) * HALF]
-                other = angles[:, :, i_lo:i_hi, (1 - f) * HALF : (2 - f) * HALF]
                 nc.scalar.activation(
-                    out=table[:, i_lo:i_hi, f, 0, :].rearrange("p i (a e) -> p i a e", a=AXES),
-                    in_=own.rearrange("p a i e -> p i a e"),
-                    func=SIN,
-                    bias=math.pi / 2,
-                    scale=-1.0,
-                )
-                nc.scalar.activation(
-                    out=table[:, i_lo:i_hi, f, 1, :].rearrange("p i (a e) -> p i a e", a=AXES),
-                    in_=other.rearrange("p a i e -> p i a e"),
+                    out=rows[:, :, 1, :, f * HALF : (f + 1) * HALF],
+                    in_=own[:, :, :, (1 - f) * HALF : (2 - f) * HALF],
                     func=SIN,
                     scale=1.0 - 2.0 * f,
                 )
@@ -194,30 +189,27 @@ def tile_attention_pa_t_kernel(
                             stop=(g == PASSES - 1),
                         )
 
+        def planes(n):
+            order = "b x i" if n + 2 * PAIR - n % PAIR >= TILES else "x i b"
+            return products[n - n % PAIR][:].rearrange(
+                "p (%s h d) -> p x i b h d" % order, x=2, i=PAIR, b=2, h=HEADS
+            )
+
         def rotate(n, parts):
             first = n - n % PAIR
             if first not in products:
-                products[first] = factors.tile([P, 2 * PAIR * BLOCK + AXIS_DIM], F32, name="products")
-            shape = [P, 2, HEADS, AXES, HALF]
+                products[first] = factors.tile([P, 2 * PAIR * 2 * PART], F32, name="products")
+            shape = [P, 2, HEADS, HEAD_DIM]
             for part in parts:
-                start = (part * PAIR + n - first) * BLOCK
-                for f in range(2):
-                    step = PART + (1 - 2 * f) * HALF
-                    lo = start + f * HALF
-                    nc.vector.tensor_tensor(
-                        out=products[first][:, lo : lo + 2 * step]
-                        .rearrange("p (u k e) -> p u k e", u=2, e=HALF)[:, :, 0 : 2 * HEADS * AXES - 1 : 2, :]
-                        .rearrange("p u (h a) e -> p u h a e", h=HEADS),
-                        in0=banks[n, part][:]
-                        .rearrange("p (h a f e) -> p h a f e", h=HEADS, a=AXES, f=2)[:, :, :, f, :]
-                        .unsqueeze(1)
-                        .to_broadcast(shape),
-                        in1=table[:, n % ROWS, f, :, :]
-                        .rearrange("p u (a e) -> p u a e", a=AXES)
-                        .unsqueeze(2)
-                        .to_broadcast(shape),
-                        op=MULT,
-                    )
+                nc.vector.tensor_tensor(
+                    out=planes(n)[:, :, n - first, part, :, :],
+                    in0=banks[n, part][:]
+                    .rearrange("p (h d) -> p h d", h=HEADS)
+                    .unsqueeze(1)
+                    .to_broadcast(shape),
+                    in1=table[:, n % ROWS, :, :].unsqueeze(2).to_broadcast(shape),
+                    op=MULT,
+                )
 
         def keep_v(n):
             if n % GROUP == 0:
@@ -232,15 +224,15 @@ def tile_attention_pa_t_kernel(
             m, lo = divmod(n, GROUP)
             if m not in rotated:
                 rotated[m] = results.tile([P, 2 * HEADS, GROUP, HEAD_DIM], F32, name="rotated")
-            both = products[first][:, 0 : 2 * PAIR * BLOCK].rearrange(
-                "p (b i t h d) -> p t i b h d", b=2, i=PAIR, t=2, h=HEADS
-            )[:, :, n - first : n - first + count, parts, :, :]
+            both = planes(n)[:, :, n - first : n - first + count, parts, :, :].rearrange(
+                "p x i b h (a f e) -> p x i b h a f e", a=AXES, f=2
+            )
             engine.tensor_tensor(
-                out=rotated[m][:, :, lo : lo + count, :].rearrange("p (b h) i d -> p i b h d", b=2)[
-                    :, :, parts, :, :
-                ],
-                in0=both[:, 0, :, :, :, :],
-                in1=both[:, 1, :, :, :, :],
+                out=rotated[m][:, :, lo : lo + count, :].rearrange(
+                    "p (b h) i (a f e) -> p i b h a f e", b=2, a=AXES, f=2
+                )[:, :, parts, :, :, :, :],
+                in0=both[:, 0, :, :, :, :, :, :],
+                in1=both[:, 1, :, :, :, :, ::-1, :],
                 op=ADD,
             )
 
@@ -293,9 +285,10 @@ def tile_attention_pa_t_kernel(
                     add_up((nc.gpsimd, nc.vector)[part], n, PAIR, slice(part, part + 1))
             else:
                 rotate(n, (0, 1))
+                rotate(n + 1, (0,))
                 if n == PAIR:
                     quantise(coming[0], PAIR)
-                rotate(n + 1, (0, 1))
+                rotate(n + 1, (1,))
                 if n + 2 * PAIR == TILES:
                     add_up(nc.vector, n, PAIR, slice(1, 2))
                     add_up(nc.gpsimd, n, PAIR, slice(0, 1))

@@ -195,16 +195,16 @@ def tile_attention_pa_t_kernel(
                 "p (%s h d) -> p x i b h d" % order, x=2, i=PAIR, b=2, h=HEADS
             )
 
-        def rotate(n, parts):
+        def rotate(n, parts, heads=slice(0, HEADS)):
             first = n - n % PAIR
             if first not in products:
                 products[first] = factors.tile([P, 2 * PAIR * 2 * PART], F32, name="products")
-            shape = [P, 2, HEADS, HEAD_DIM]
+            shape = [P, 2, heads.stop - heads.start, HEAD_DIM]
             for part in parts:
                 nc.vector.tensor_tensor(
-                    out=planes(n)[:, :, n - first, part, :, :],
+                    out=planes(n)[:, :, n - first, part, heads, :],
                     in0=banks[n, part][:]
-                    .rearrange("p (h d) -> p h d", h=HEADS)
+                    .rearrange("p (h d) -> p h d", h=HEADS)[:, heads, :]
                     .unsqueeze(1)
                     .to_broadcast(shape),
                     in1=table[:, n % ROWS, :, :].unsqueeze(2).to_broadcast(shape),
@@ -270,42 +270,52 @@ def tile_attention_pa_t_kernel(
             keep_v(n + 1)
             for t in ahead:
                 transpose(t)
-            if n > PAIR and coming:
-                quantise(coming[0], PAIR)
+                regroup(t)
             if n == 0:
                 rotate(n, (0, 1))
                 quantise(coming[0], 1)
                 rotate(n + 1, (0, 1))
                 quantise(coming[1], 1)
                 add_up(nc.gpsimd, n, PAIR, slice(0, 2))
-            elif last:
-                for part in range(2):
-                    for t in (n, n + 1):
-                        rotate(t, (part,))
-                    add_up((nc.gpsimd, nc.vector)[part], n, PAIR, slice(part, part + 1))
-            else:
+            elif n == PAIR:
                 rotate(n, (0, 1))
                 rotate(n + 1, (0,))
-                if n == PAIR:
+                quantise(coming[0], PAIR)
+                rotate(n + 1, (1,), slice(0, HEADS - 1))
+                quantise(ahead[0], PAIR)
+                rotate(n + 1, (1,), slice(HEADS - 1, HEADS))
+                add_up(nc.gpsimd, n, PAIR, slice(0, 2))
+            elif n + 2 * PAIR < TILES:
+                if n > 2 * PAIR:
                     quantise(coming[0], PAIR)
+                rotate(n, (0, 1))
+                rotate(n + 1, (0, 1))
+                add_up(nc.gpsimd, n, PAIR, slice(0, 2))
+            else:
+                if coming:
+                    quantise(coming[0], PAIR)
+                rotate(n, (0,))
+                rotate(n + 1, (0,))
+                if last:
+                    add_up(nc.vector, n - PAIR, PAIR, slice(1, 2))
+                add_up(nc.gpsimd, n, PAIR, slice(0, 1))
+                rotate(n, (1,))
                 rotate(n + 1, (1,))
-                if n + 2 * PAIR == TILES:
+                if last:
                     add_up(nc.vector, n, PAIR, slice(1, 2))
-                    add_up(nc.gpsimd, n, PAIR, slice(0, 1))
-                else:
-                    add_up(nc.gpsimd, n, PAIR, slice(0, 2))
             if n + 2 * GROUP >= TILES:
                 store(n, PAIR, (2,))
             elif (n + PAIR) % GROUP == 0:
                 store(n + PAIR - GROUP, GROUP, (2,))
-            for t in ahead:
-                regroup(t)
             if n + 3 * PAIR < TILES:
                 sort_words(n + 3 * PAIR)
             if n + GROUP < ROWS:
                 make_table(n + GROUP, n + GROUP + PAIR)
             if n + 2 * PAIR == TILES:
-                store(n, PAIR, (1, 0))
+                store(n, PAIR, (0,))
+            elif last:
+                store(n - PAIR, PAIR, (1,))
+                store(n, PAIR, (0, 1))
             elif n + 2 * GROUP >= TILES:
                 store(n, PAIR, (0, 1))
             elif (n + PAIR) % GROUP == 0:

import math
from contextlib import ExitStack

import concourse.mybir as mybir
from concourse.masks import make_identity

F32 = mybir.dt.float32
BF16 = mybir.dt.bfloat16
I32 = mybir.dt.int32
U8 = mybir.dt.uint8
U32 = mybir.dt.uint32
FP8X4 = mybir.dt.float8_e4m3fn_x4
FP4X4 = mybir.dt.float4_e2m1fn_x4
MULT = mybir.AluOpType.mult
ADD = mybir.AluOpType.add
SIN = mybir.ActivationFunctionType.Sin

P = 128
BATCH, TOKENS, DIM = 2, 2048, 1024
HEADS, HEAD_DIM = 4, 96
AXES, AXIS_DIM = 3, 32
PART = HEADS * HEAD_DIM
PACK = 4
PASSES = DIM // (P * PACK)
WORDS = P * PACK // 2
CHUNK = 128
ROWS = TOKENS // P
TILES = BATCH * ROWS
PAIR = 2
GROUP = 4
UNSORTED = 3 * PAIR
HALF = AXIS_DIM // 2
WARM_UP = 16
KEEP_WARM = 6

FLOPS = 2 * BATCH * TOKENS * DIM * 3 * PART


def tile_attention_pa_t_kernel(
    tc, x, f1, f2, f3, Wqkv_words, Wqkv_scales, out_0, out_1, out_2
):
    nc = tc.nc
    x_rows = x.rearrange("b (p i) k -> b p i k", i=ROWS)
    out_rows = [o.rearrange("b h (p i) d -> b p h i d", i=ROWS) for o in (out_0, out_1, out_2)]

    with ExitStack() as ctx:
        const = ctx.enter_context(tc.tile_pool(name="const", bufs=1))
        x_pool = ctx.enter_context(tc.tile_pool(name="x_pool", bufs=TILES // PAIR))
        stage = ctx.enter_context(tc.tile_pool(name="stage", bufs=3))
        sorting = ctx.enter_context(tc.tile_pool(name="sorting", bufs=2))
        results = ctx.enter_context(tc.tile_pool(name="results", bufs=3))
        factors = ctx.enter_context(tc.tile_pool(name="factors", bufs=3))
        psum_t = ctx.enter_context(tc.psum_pool(name="psum_t", bufs=PAIR))
        psum_o = ctx.enter_context(tc.psum_pool(name="psum_o", bufs=PAIR))
        ctx.enter_context(tc.manual_schedule())

        ident = const.tile([P, P], F32, name="ident")
        make_identity(nc, ident[:])
        angles = const.tile([P, AXES, ROWS, AXIS_DIM], BF16, name="angles")
        cold = const.tile([P, P], BF16, name="cold")
        nc.vector.memset(cold[:], 0.0)

        w_scales = const.tile([P, PASSES, 3 * PART], U8, name="w_scales", align_bytes=64)
        nc.vector.memset(w_scales[:].bitcast(I32), 0)
        w_words = const.tile([P, PASSES, 2 * 3 * PART], U8, name="w_words", align_bytes=64)
        table = const.tile([P, ROWS, 2, HEAD_DIM], F32, name="table")

        zero = const.tile([P, 1], F32, name="zero")
        nc.vector.memset(zero[:], 0.0)
        nc.scalar.activation(out=zero[:], in_=zero[:], func=SIN)

        warmth = psum_t.tile([P, PASSES, 2, P], F32, name="flipped")
        for turn in range(WARM_UP):
            nc.tensor.matmul(
                out=warmth[:, 0, 0, :],
                lhsT=cold[:],
                rhs=cold[:],
                start=True,
                stop=True,
            )

        x_tiles = {}

        def load_x(n, count):
            first = n - n % PAIR
            if n == first:
                x_tiles[first] = x_pool.tile([P, PAIR, DIM], BF16, name="x_pair")
            b, i0 = divmod(n, ROWS)
            nc.sync.dma_start(
                out=x_tiles[first][:, n - first : n - first + count, :],
                in_=x_rows[b][:, i0 : i0 + count, :],
            )

        load_x(0, 1)
        load_x(1, 1)
        scale_rows = Wqkv_scales.rearrange("g (q r) n -> r q g n", r=4)
        for r in range(4):
            nc.sync.dma_start(
                out=w_scales[r:P:32, :, :].bitcast(I32), in_=scale_rows[r].bitcast(I32)
            )
        nc.sync.dma_start(
            out=w_words[:].bitcast(I32), in_=Wqkv_words.rearrange("g p n -> p g n").bitcast(I32)
        )
        for a, f in enumerate((f1, f2, f3)):
            nc.sync.dma_start(
                out=angles[:, a, :, :], in_=f.rearrange("(p i) e -> p i e", i=ROWS)
            )
        load_x(PAIR, 1)
        load_x(PAIR + 1, 1)
        for n in range(2 * PAIR, TILES, PAIR):
            load_x(n, PAIR)

        def make_table(i_lo, i_hi):
            own = angles[:, :, i_lo:i_hi, :].rearrange("p a i e -> p i a e")
            rows = table[:, i_lo:i_hi, :, :].rearrange("p i u (a e) -> p i u a e", a=AXES)
            nc.scalar.activation(
                out=rows[:, :, 0, :, :], in_=own, func=SIN, bias=math.pi / 2, scale=-1.0
            )
            for f in range(2):
                nc.scalar.activation(
                    out=rows[:, :, 1, :, f * HALF : (f + 1) * HALF],
                    in_=own[:, :, :, (1 - f) * HALF : (2 - f) * HALF],
                    func=SIN,
                    scale=1.0 - 2.0 * f,
                )

        ordered, flipped, grouped, codes, x_scales = {}, {}, {}, {}, {}
        banks, products, rotated, v_rows = {}, {}, {}, {}

        def sort_words(n):
            ordered[n] = sorting.tile([P, PAIR, PASSES, 2, P], F32, name="ordered")
            nc.scalar.copy(
                out=ordered[n][:].rearrange("p e g u q -> p (e g) u q"),
                in_=x_tiles[n][:]
                .bitcast(F32)
                .rearrange("p e (g q u) -> p (e g) u q", g=PASSES, u=2),
            )

        def transpose(n):
            flipped[n] = psum_t.tile([P, PASSES, 2, P], F32, name="flipped")
            words = x_tiles[n - n % PAIR][:, n % PAIR, :].bitcast(F32)
            for g in range(PASSES):
                for u in range(2):
                    if n < UNSORTED:
                        columns = words[:, WORDS * g + u : WORDS * (g + 1) : 2]
                    else:
                        columns = ordered[n - n % PAIR][:, n % PAIR, g, u, :]
                    nc.tensor.transpose(flipped[n][:, g, u, :], columns, ident[:])

        def regroup(n):
            first = n - n % PAIR
            if n == first:
                grouped[first] = stage.tile(
                    [P, PAIR, PASSES, P, PACK], BF16, name="grouped", align_bytes=64
                )
            nc.scalar.copy(
                out=grouped[first][:, n - first, :, :, :].bitcast(F32),
                in_=flipped[n][:].rearrange("p g u r -> p g r u"),
            )

        def quantise(n, count):
            first = n - n % PAIR
            if n == first:
                codes[first] = stage.tile([P, PAIR, PASSES, P], U32, name="codes", align_bytes=64)
                x_scales[first] = stage.tile(
                    [P, PAIR, PASSES, P], U8, name="x_scales", align_bytes=64
                )
            lo, hi = n - first, n - first + count
            nc.vector.quantize_mx(
                out=codes[first][:, lo:hi, :, :].rearrange("p e g r -> p (e g r)").bitcast(FP8X4),
                scales=x_scales[first][:, lo:hi, :, :].rearrange("p e g r -> p (e g r)"),
                in_=grouped[first][:, lo:hi, :, :, :].rearrange("p e g r t -> p (e g r t)"),
            )

        def project(n):
            for part in range(3):
                bank = psum_o.tile([P, PART], F32, name="bank%d" % part)
                banks[n, part] = bank
                for c in range(PART // CHUNK):
                    col = part * PART + c * CHUNK
                    for g in range(PASSES):
                        nc.tensor.matmul_mx(
                            out=bank[:, c * CHUNK : (c + 1) * CHUNK],
                            lhsT=codes[n - n % PAIR][:, n % PAIR, g, :].bitcast(FP8X4),
                            lhsT_scale=x_scales[n - n % PAIR][:, n % PAIR, g, :],
                            rhs=w_words[:, g, 2 * col : 2 * (col + CHUNK)].bitcast(FP4X4),
                            rhs_scale=w_scales[:, g, col : col + CHUNK],
                            start=(g == 0),
                            stop=(g == PASSES - 1),
                        )

        def planes(n):
            order = "b x i" if n + 2 * PAIR - n % PAIR >= TILES else "x i b"
            return products[n - n % PAIR][:].rearrange(
                "p (%s h d) -> p x i b h d" % order, x=2, i=PAIR, b=2, h=HEADS
            )

        def rotate(n, parts, heads=slice(0, HEADS)):
            first = n - n % PAIR
            if first not in products:
                products[first] = factors.tile([P, 2 * PAIR * 2 * PART], F32, name="products")
            shape = [P, 2, heads.stop - heads.start, HEAD_DIM]
            for part in parts:
                nc.vector.tensor_tensor(
                    out=planes(n)[:, :, n - first, part, heads, :],
                    in0=banks[n, part][:]
                    .rearrange("p (h d) -> p h d", h=HEADS)[:, heads, :]
                    .unsqueeze(1)
                    .to_broadcast(shape),
                    in1=table[:, n % ROWS, :, :].unsqueeze(2).to_broadcast(shape),
                    op=MULT,
                )

        def keep_v(n):
            if n % GROUP == 0:
                v_rows[n // GROUP] = results.tile([P, HEADS, GROUP, HEAD_DIM], F32, name="v_rows")
            nc.scalar.copy(
                out=v_rows[n // GROUP][:, :, n % GROUP, :],
                in_=banks[n, 2][:].rearrange("p (h d) -> p h d", h=HEADS),
            )

        def add_up(engine, n, count, parts):
            first = n - n % PAIR
            m, lo = divmod(n, GROUP)
            if m not in rotated:
                rotated[m] = results.tile([P, 2 * HEADS, GROUP, HEAD_DIM], F32, name="rotated")
            both = planes(n)[:, :, n - first : n - first + count, parts, :, :].rearrange(
                "p x i b h (a f e) -> p x i b h a f e", a=AXES, f=2
            )
            engine.tensor_tensor(
                out=rotated[m][:, :, lo : lo + count, :].rearrange(
                    "p (b h) i (a f e) -> p i b h a f e", b=2, a=AXES, f=2
                )[:, :, parts, :, :, :, :],
                in0=both[:, 0, :, :, :, :, :, :],
                in1=both[:, 1, :, :, :, :, ::-1, :],
                op=ADD,
            )

        def store(n, count, parts):
            m, lo = divmod(n, GROUP)
            b, i0 = divmod(n, ROWS)
            for part in parts:
                if part == 2:
                    rows = v_rows[m][:, :, lo : lo + count, :]
                else:
                    rows = rotated[m][:, part * HEADS : (part + 1) * HEADS, lo : lo + count, :]
                queue = nc.scalar if part == 2 and n + 2 * GROUP >= TILES else nc.sync
                queue.dma_start(out=out_rows[part][b][:, :, i0 : i0 + count, :], in_=rows)

        idle = psum_o.tile([P, PART], F32, name="bank2")
        for n in range(PAIR):
            transpose(n)
            for turn in range(KEEP_WARM):
                nc.tensor.matmul(out=idle[:, 0:P], lhsT=cold[:], rhs=cold[:], start=True, stop=True)
            regroup(n)
            quantise(n, 1)
        make_table(0, PAIR)
        make_table(PAIR, GROUP)
        for n in range(0, TILES, PAIR):
            coming = [t for t in (n + PAIR, n + PAIR + 1) if t < TILES]
            ahead = [t for t in (n + 2 * PAIR, n + 2 * PAIR + 1) if t < TILES]
            last = n + PAIR == TILES
            project(n)
            keep_v(n)
            if n == 0:
                for t in coming:
                    transpose(t)
                    regroup(t)
            project(n + 1)
            keep_v(n + 1)
            for t in ahead:
                transpose(t)
                regroup(t)
            if n == 0:
                rotate(n, (0, 1))
                quantise(coming[0], 1)
                rotate(n + 1, (0, 1))
                quantise(coming[1], 1)
                add_up(nc.gpsimd, n, PAIR, slice(0, 2))
            elif n == PAIR:
                rotate(n, (0, 1))
                rotate(n + 1, (0,))
                quantise(coming[0], PAIR)
                rotate(n + 1, (1,), slice(0, HEADS - 1))
                quantise(ahead[0], PAIR)
                rotate(n + 1, (1,), slice(HEADS - 1, HEADS))
                add_up(nc.gpsimd, n, PAIR, slice(0, 2))
            elif n + 2 * PAIR < TILES:
                if n > 2 * PAIR:
                    quantise(coming[0], PAIR)
                rotate(n, (0, 1))
                rotate(n + 1, (0, 1))
                add_up(nc.gpsimd, n, PAIR, slice(0, 2))
            else:
                if coming:
                    quantise(coming[0], PAIR)
                rotate(n, (0,))
                rotate(n + 1, (0,))
                if last:
                    add_up(nc.vector, n - PAIR, PAIR, slice(1, 2))
                add_up(nc.gpsimd, n, PAIR, slice(0, 1))
                rotate(n, (1,))
                rotate(n + 1, (1,))
                if last:
                    add_up(nc.vector, n, PAIR, slice(1, 2))
            if n + 2 * GROUP >= TILES:
                store(n, PAIR, (2,))
            elif (n + PAIR) % GROUP == 0:
                store(n + PAIR - GROUP, GROUP, (2,))
            if n + 3 * PAIR < TILES:
                sort_words(n + 3 * PAIR)
            if n + GROUP < ROWS:
                make_table(n + GROUP, n + GROUP + PAIR)
            if n + 2 * PAIR == TILES:
                store(n, PAIR, (0,))
            elif last:
                store(n - PAIR, PAIR, (1,))
                store(n, PAIR, (0, 1))
            elif n + 2 * GROUP >= TILES:
                store(n, PAIR, (0, 1))
            elif (n + PAIR) % GROUP == 0:
                store(n + PAIR - GROUP, GROUP, (0, 1))
